import numpy as np
import ml_dtypes


def mxq(x, axis, fmt="e4m3"):
    dtype, down = {"e4m3": (ml_dtypes.float8_e4m3fn, 7), "e5m2": (ml_dtypes.float8_e5m2, 14)}[fmt]
    v = np.moveaxis(np.asarray(x, np.float32).astype(ml_dtypes.bfloat16).astype(np.float64), axis, -1)
    blocks = v.reshape(v.shape[:-1] + (-1, 32))
    amax = np.abs(blocks).max(-1, keepdims=True)
    byte = np.maximum(np.where(amax > 0, np.frexp(amax)[1] - 1 + 127, 0) - down, 1)
    scale = np.exp2(byte - 127.0)
    codes = (blocks / scale).astype(np.float32).astype(dtype).astype(np.float64)
    return np.moveaxis((codes * scale).reshape(v.shape), -1, axis)


WIDE = False


def mx_kscale(k):
    if not WIDE:
        return np.ones(k)
    levels = np.array([10, -10, 5, -5, 0])
    a = np.random.permutation(np.resize(levels, k // 512 * 4)).reshape(k // 512, 4)
    idx = np.arange(k)
    return np.exp2(a[idx // 512, idx % 128 // 32])


BF16 = ml_dtypes.bfloat16


def bf(x):
    return np.asarray(x, np.float32).astype(BF16)


def f64(x):
    return np.asarray(x).astype(np.float64)


B, T, D, H = 16, 128, 512, 8
NEG_INF = -1e30


def setup_inputs():
    s = mx_kscale(D)
    return {"h": bf(np.random.standard_normal((B, T, D)) * s),
            "A": bf(np.random.standard_normal((H, D, D)) * 3.0 / D / s[:, None] / s[None, :])}


def reference(h, A):
    hq = mxq(f64(h), 2, "e4m3")
    hA = hq[:, None, 1:] @ mxq(f64(A), 1, "e4m3")[None]
    rest = mxq(hA, 3, "e4m3") @ hq[:, None].transpose(0, 1, 3, 2)
    scores = np.concatenate([np.zeros((B, H, 1, T)), rest], axis=2)
    causal = np.tril(np.ones((T, T), dtype=bool))
    scores = np.where(causal, scores, NEG_INF)
    e = np.exp(scores - scores.max(-1, keepdims=True))
    return e / e.sum(-1, keepdims=True)

@@ -1,0 +1,142 @@
+from contextlib import ExitStack
+
+import concourse.mybir as mybir
+from concourse.masks import make_identity
+
+FP8X4 = mybir.dt.float8_e4m3fn_x4
+BF16 = mybir.dt.bfloat16
+F32 = mybir.dt.float32
+U32 = mybir.dt.uint32
+U8 = mybir.dt.uint8
+ALU = mybir.AluOpType
+ACT = mybir.ActivationFunctionType
+AXIS = mybir.AxisListType
+
+B, T, D, H = 16, 128, 512, 8
+P = 128
+PACK = 4
+NEG_INF = -1e30
+HEADS_PER_BANK = 4
+BATCHES_PER_LOAD = 4
+
+FLOPS = 2 * B * H * T * D * (D + T)
+
+
+def tile_causalselfattention_pa_kernel(tc, h, A, out):
+    nc = tc.nc
+    with ExitStack() as ctx:
+        const = ctx.enter_context(tc.tile_pool(name="const", bufs=1))
+        a_stage = ctx.enter_context(tc.tile_pool(name="a_stage", bufs=3))
+        ha_stage = ctx.enter_context(tc.tile_pool(name="ha_stage", bufs=4))
+        soft = ctx.enter_context(tc.tile_pool(name="soft", bufs=4))
+        psum_t = ctx.enter_context(tc.psum_pool(name="psum_t", bufs=2))
+        psum_ha = ctx.enter_context(tc.psum_pool(name="psum_ha", bufs=4))
+        psum_sc = ctx.enter_context(tc.psum_pool(name="psum_sc", bufs=2))
+
+        ident = const.tile([P, P], BF16)
+        make_identity(nc, ident[:])
+        mask = const.tile([P, T], F32)
+        nc.gpsimd.memset(mask[:], 0.0)
+        nc.gpsimd.affine_select(
+            out=mask[:], in_=mask[:], compare_op=ALU.is_ge, fill=NEG_INF,
+            base=0, pattern=[[-1, T]], channel_multiplier=1,
+        )
+
+        h_raw = const.tile([P, B, D], BF16)
+        for b0 in range(0, B, BATCHES_PER_LOAD):
+            nc.sync.dma_start(
+                out=h_raw[:, b0 : b0 + BATCHES_PER_LOAD, :],
+                in_=h[b0 : b0 + BATCHES_PER_LOAD].rearrange("b t d -> t b d"),
+            )
+
+        h_grouped = const.tile([P, B, T, PACK], BF16, align_bytes=64)
+        h_codes = const.tile([P, B, T], U32, align_bytes=64)
+        h_scales = const.tile([P, B, T], U8, align_bytes=64)
+        for b0 in range(0, B, BATCHES_PER_LOAD):
+            for b in range(b0, b0 + BATCHES_PER_LOAD):
+                h_t = psum_t.tile([P, PACK, T], BF16)
+                for c in range(PACK):
+                    nc.tensor.transpose(h_t[:, c, :], h_raw[:, b, c * P : (c + 1) * P], ident[:])
+                nc.any.tensor_copy(out=h_grouped[:, b, :, :], in_=h_t[:].rearrange("p c t -> p t c"))
+            group = slice(b0, b0 + BATCHES_PER_LOAD)
+            nc.vector.quantize_mx(
+                out=h_codes[:, group, :].rearrange("p b t -> p (b t)").bitcast(FP8X4),
+                scales=h_scales[:, group, :].rearrange("p b t -> p (b t)"),
+                in_=h_grouped[:, group, :, :].rearrange("p b t c -> p (b t c)"),
+            )
+
+        a_codes = const.tile([P, H, D], U32, align_bytes=64)
+        a_scales = const.tile([P, H, D], U8, align_bytes=64)
+        for n in range(H):
+            a_raw = a_stage.tile([P, PACK, D], BF16)
+            nc.sync.dma_start(out=a_raw[:], in_=A[n].rearrange("(c p) e -> p c e", p=P))
+            a_grouped = a_stage.tile([P, D, PACK], BF16, align_bytes=64)
+            nc.vector.tensor_copy(
+                out=a_grouped[:].rearrange("p (e i) c -> p e c i", i=4),
+                in_=a_raw[:].rearrange("p c (e i) -> p e c i", i=4),
+            )
+            nc.vector.quantize_mx(
+                out=a_codes[:, n, :].bitcast(FP8X4),
+                scales=a_scales[:, n, :],
+                in_=a_grouped[:].rearrange("p e c -> p (e c)"),
+            )
+
+        for b in range(B):
+            ha_grouped = ha_stage.tile([P, H, T, PACK], BF16, align_bytes=64)
+            for n in range(H):
+                ha_t = psum_ha.tile([P, PACK, T], F32)
+                for c in range(PACK):
+                    e_cols = slice(c * P, (c + 1) * P)
+                    nc.tensor.matmul_mx(
+                        out=ha_t[:, c, :],
+                        lhsT=a_codes[:, n, e_cols].bitcast(FP8X4),
+                        lhsT_scale=a_scales[:, n, e_cols],
+                        rhs=h_codes[:, b, :].bitcast(FP8X4),
+                        rhs_scale=h_scales[:, b, :],
+                        start=True,
+                        stop=True,
+                    )
+                nc.any.tensor_copy(out=ha_grouped[:, n, :, :], in_=ha_t[:].rearrange("p c t -> p t c"))
+            ha_codes = ha_stage.tile([P, H, T], U32, align_bytes=64)
+            ha_scales = ha_stage.tile([P, H, T], U8, align_bytes=64)
+            nc.vector.quantize_mx(
+                out=ha_codes[:].rearrange("p n t -> p (n t)").bitcast(FP8X4),
+                scales=ha_scales[:].rearrange("p n t -> p (n t)"),
+                in_=ha_grouped[:].rearrange("p n t c -> p (n t c)"),
+            )
+
+            for n0 in range(0, H, HEADS_PER_BANK):
+                scores = psum_sc.tile([P, HEADS_PER_BANK, T], F32)
+                for g in range(HEADS_PER_BANK):
+                    nc.tensor.matmul_mx(
+                        out=scores[:, g, :],
+                        lhsT=ha_codes[:, n0 + g, :].bitcast(FP8X4),
+                        lhsT_scale=ha_scales[:, n0 + g, :],
+                        rhs=h_codes[:, b, :].bitcast(FP8X4),
+                        rhs_scale=h_scales[:, b, :],
+                        start=True,
+                        stop=True,
+                    )
+                masked = soft.tile([P, HEADS_PER_BANK, T], F32)
+                nc.vector.tensor_tensor(
+                    out=masked[:], in0=scores[:],
+                    in1=mask[:].unsqueeze(1).to_broadcast([P, HEADS_PER_BANK, T]), op=ALU.add,
+                )
+                neg_max = soft.tile([P, HEADS_PER_BANK], F32)
+                nc.vector.tensor_reduce(out=neg_max[:], in_=masked[:], axis=AXIS.X, op=ALU.max, negate=True)
+                attn = soft.tile([P, HEADS_PER_BANK, T], F32)
+                row_sum = soft.tile([P, HEADS_PER_BANK], F32)
+                for g in range(HEADS_PER_BANK):
+                    nc.scalar.activation(
+                        out=attn[:, g, :], in_=masked[:, g, :], func=ACT.Exp,
+                        bias=neg_max[:, g : g + 1], scale=1.0, accum_out=row_sum[:, g : g + 1],
+                    )
+                inv_sum = soft.tile([P, HEADS_PER_BANK], F32)
+                nc.vector.reciprocal(out=inv_sum[:], in_=row_sum[:])
+                nc.vector.tensor_tensor(
+                    out=attn[:], in0=attn[:],
+                    in1=inv_sum[:].unsqueeze(2).to_broadcast([P, HEADS_PER_BANK, T]), op=ALU.mult,
+                )
+                nc.sync.dma_start(
+                    out=out[b, n0 : n0 + HEADS_PER_BANK].rearrange("n t s -> t n s"), in_=attn[:]
+                )

@@ -16,8 +16,15 @@ B, T, D, H = 16, 128, 512, 8
 P = 128
 PACK = 4
 NEG_INF = -1e30
-HEADS_PER_BANK = 4
-BATCHES_PER_LOAD = 4
+CHUNK = 4
+
+BLOCK = 32
+N_BLOCKS = T // BLOCK
+STACK = P // BLOCK
+N_STACKS = H // STACK
+TILES_PER_BANK = 4
+BATCHES_PER_BANK = TILES_PER_BANK // N_STACKS
+ATTN_BUFS = 3
 
 FLOPS = 2 * B * H * T * D * (D + T)
 
@@ -33,47 +40,68 @@ def tile_causalselfattention_pa_kernel(tc, h, A, out):
         psum_ha = ctx.enter_context(tc.psum_pool(name="psum_ha", bufs=4))
         psum_sc = ctx.enter_context(tc.psum_pool(name="psum_sc", bufs=2))
 
+        h_raw = const.tile([P, B, D], BF16)
+        a_raw = const.tile([P, H, PACK, D], BF16)
+
+        def load_h(b0):
+            nc.sync.dma_start(
+                out=h_raw[:, b0 : b0 + CHUNK, :], in_=h[b0 : b0 + CHUNK].rearrange("b t d -> t b d")
+            )
+
+        load_h(0)
+        for n in range(H):
+            nc.sync.dma_start(out=a_raw[:, n, :, :], in_=A[n].rearrange("(c p) e -> p c e", p=P))
+        for b0 in range(CHUNK, B, CHUNK):
+            load_h(b0)
+
         ident = const.tile([P, P], BF16)
         make_identity(nc, ident[:])
-        mask = const.tile([P, T], F32)
-        nc.gpsimd.memset(mask[:], 0.0)
-        nc.gpsimd.affine_select(
-            out=mask[:], in_=mask[:], compare_op=ALU.is_ge, fill=NEG_INF,
-            base=0, pattern=[[-1, T]], channel_multiplier=1,
-        )
+        ident_f32 = const.tile([P, P], F32)
+        make_identity(nc, ident_f32[:])
 
-        h_raw = const.tile([P, B, D], BF16)
-        for b0 in range(0, B, BATCHES_PER_LOAD):
-            nc.sync.dma_start(
-                out=h_raw[:, b0 : b0 + BATCHES_PER_LOAD, :],
-                in_=h[b0 : b0 + BATCHES_PER_LOAD].rearrange("b t d -> t b d"),
-            )
+        mask_t = const.tile([P, P], F32)
+        nc.gpsimd.memset(mask_t[:], 0.0)
+        nc.gpsimd.affine_select(
+            out=mask_t[:], in_=mask_t[:], compare_op=ALU.is_ge, fill=NEG_INF,
+            base=T - BLOCK, channel_multiplier=-1, pattern=[[0, STACK], [1, BLOCK]],
+        )
+        mask_ps = psum_t.tile([P, P], F32, tag="transposed")
+        nc.tensor.transpose(mask_ps[:], mask_t[:], ident_f32[:])
+        mask = const.tile([P, T], F32)
+        nc.vector.tensor_copy(out=mask[:], in_=mask_ps[:])
+
+        attn_tiles = {}
+        for j in range(N_BLOCKS):
+            for k in range(ATTN_BUFS):
+                attn_tile = const.tile([P, TILES_PER_BANK, T], F32, name="attn_%d_%d" % (j, k))
+                if j < N_BLOCKS - 1:
+                    nc.gpsimd.memset(attn_tile[:, :, BLOCK * (j + 1) :], 0.0)
+                attn_tiles[(j, k)] = attn_tile
 
         h_grouped = const.tile([P, B, T, PACK], BF16, align_bytes=64)
         h_codes = const.tile([P, B, T], U32, align_bytes=64)
         h_scales = const.tile([P, B, T], U8, align_bytes=64)
-        for b0 in range(0, B, BATCHES_PER_LOAD):
-            for b in range(b0, b0 + BATCHES_PER_LOAD):
-                h_t = psum_t.tile([P, PACK, T], BF16)
+        a_codes = const.tile([P, H, D], U32, align_bytes=64)
+        a_scales = const.tile([P, H, D], U8, align_bytes=64)
+
+        def prepare_h(b0):
+            for b in range(b0, b0 + CHUNK):
+                h_t = psum_t.tile([P, PACK, T], BF16, tag="transposed")
                 for c in range(PACK):
                     nc.tensor.transpose(h_t[:, c, :], h_raw[:, b, c * P : (c + 1) * P], ident[:])
                 nc.any.tensor_copy(out=h_grouped[:, b, :, :], in_=h_t[:].rearrange("p c t -> p t c"))
-            group = slice(b0, b0 + BATCHES_PER_LOAD)
+            chunk = slice(b0, b0 + CHUNK)
             nc.vector.quantize_mx(
-                out=h_codes[:, group, :].rearrange("p b t -> p (b t)").bitcast(FP8X4),
-                scales=h_scales[:, group, :].rearrange("p b t -> p (b t)"),
-                in_=h_grouped[:, group, :, :].rearrange("p b t c -> p (b t c)"),
+                out=h_codes[:, chunk, :].rearrange("p b t -> p (b t)").bitcast(FP8X4),
+                scales=h_scales[:, chunk, :].rearrange("p b t -> p (b t)"),
+                in_=h_grouped[:, chunk, :, :].rearrange("p b t c -> p (b t c)"),
             )
 
-        a_codes = const.tile([P, H, D], U32, align_bytes=64)
-        a_scales = const.tile([P, H, D], U8, align_bytes=64)
-        for n in range(H):
-            a_raw = a_stage.tile([P, PACK, D], BF16)
-            nc.sync.dma_start(out=a_raw[:], in_=A[n].rearrange("(c p) e -> p c e", p=P))
+        def prepare_a(n):
             a_grouped = a_stage.tile([P, D, PACK], BF16, align_bytes=64)
             nc.vector.tensor_copy(
                 out=a_grouped[:].rearrange("p (e i) c -> p e c i", i=4),
-                in_=a_raw[:].rearrange("p c (e i) -> p e c i", i=4),
+                in_=a_raw[:, n, :, :].rearrange("p c (e i) -> p e c i", i=4),
             )
             nc.vector.quantize_mx(
                 out=a_codes[:, n, :].bitcast(FP8X4),
@@ -81,62 +109,85 @@ def tile_causalselfattention_pa_kernel(tc, h, A, out):
                 in_=a_grouped[:].rearrange("p e c -> p (e c)"),
             )
 
-        for b in range(B):
-            ha_grouped = ha_stage.tile([P, H, T, PACK], BF16, align_bytes=64)
-            for n in range(H):
-                ha_t = psum_ha.tile([P, PACK, T], F32)
-                for c in range(PACK):
-                    e_cols = slice(c * P, (c + 1) * P)
-                    nc.tensor.matmul_mx(
-                        out=ha_t[:, c, :],
-                        lhsT=a_codes[:, n, e_cols].bitcast(FP8X4),
-                        lhsT_scale=a_scales[:, n, e_cols],
-                        rhs=h_codes[:, b, :].bitcast(FP8X4),
-                        rhs_scale=h_scales[:, b, :],
-                        start=True,
-                        stop=True,
+        def project(b):
+            ha_grouped = ha_stage.tile([P, N_STACKS, N_BLOCKS, STACK, BLOCK, PACK], BF16, align_bytes=64)
+            ha_codes = ha_stage.tile([P, N_STACKS, N_BLOCKS, P], U32, align_bytes=64)
+            ha_scales = ha_stage.tile([P, N_STACKS, N_BLOCKS, P], U8, align_bytes=64)
+            for k in range(N_STACKS):
+                for n in range(STACK):
+                    head = k * STACK + n
+                    ha_t = psum_ha.tile([P, PACK, T], F32)
+                    for c in range(PACK):
+                        e_cols = slice(c * P, (c + 1) * P)
+                        nc.tensor.matmul_mx(
+                            out=ha_t[:, c, :],
+                            lhsT=a_codes[:, head, e_cols].bitcast(FP8X4),
+                            lhsT_scale=a_scales[:, head, e_cols],
+                            rhs=h_codes[:, b, :].bitcast(FP8X4),
+                            rhs_scale=h_scales[:, b, :],
+                            start=True,
+                            stop=True,
+                        )
+                    nc.any.tensor_copy(
+                        out=ha_grouped[:, k, :, n, :, :],
+                        in_=ha_t[:].rearrange("p c (j i) -> p j i c", i=BLOCK),
                     )
-                nc.any.tensor_copy(out=ha_grouped[:, n, :, :], in_=ha_t[:].rearrange("p c t -> p t c"))
-            ha_codes = ha_stage.tile([P, H, T], U32, align_bytes=64)
-            ha_scales = ha_stage.tile([P, H, T], U8, align_bytes=64)
-            nc.vector.quantize_mx(
-                out=ha_codes[:].rearrange("p n t -> p (n t)").bitcast(FP8X4),
-                scales=ha_scales[:].rearrange("p n t -> p (n t)"),
-                in_=ha_grouped[:].rearrange("p n t c -> p (n t c)"),
-            )
+                nc.vector.quantize_mx(
+                    out=ha_codes[:, k, :, :].rearrange("p j r -> p (j r)").bitcast(FP8X4),
+                    scales=ha_scales[:, k, :, :].rearrange("p j r -> p (j r)"),
+                    in_=ha_grouped[:, k, :, :, :, :].rearrange("p j n i c -> p (j n i c)"),
+                )
+            return ha_codes, ha_scales
 
-            for n0 in range(0, H, HEADS_PER_BANK):
-                scores = psum_sc.tile([P, HEADS_PER_BANK, T], F32)
-                for g in range(HEADS_PER_BANK):
-                    nc.tensor.matmul_mx(
-                        out=scores[:, g, :],
-                        lhsT=ha_codes[:, n0 + g, :].bitcast(FP8X4),
-                        lhsT_scale=ha_scales[:, n0 + g, :],
-                        rhs=h_codes[:, b, :].bitcast(FP8X4),
-                        rhs_scale=h_scales[:, b, :],
-                        start=True,
-                        stop=True,
-                    )
-                masked = soft.tile([P, HEADS_PER_BANK, T], F32)
-                nc.vector.tensor_tensor(
-                    out=masked[:], in0=scores[:],
-                    in1=mask[:].unsqueeze(1).to_broadcast([P, HEADS_PER_BANK, T]), op=ALU.add,
+        def attend(b0, quantised, j, attn):
+            width = BLOCK * (j + 1)
+            scores = psum_sc.tile([P, TILES_PER_BANK, T], F32)
+            for g in range(TILES_PER_BANK):
+                ha_codes, ha_scales = quantised[g // N_STACKS]
+                b = b0 + g // N_STACKS
+                nc.tensor.matmul_mx(
+                    out=scores[:, g, :],
+                    lhsT=ha_codes[:, g % N_STACKS, j, :].bitcast(FP8X4),
+                    lhsT_scale=ha_scales[:, g % N_STACKS, j, :],
+                    rhs=h_codes[:, b, :].bitcast(FP8X4),
+                    rhs_scale=h_scales[:, b, :],
+                    start=True,
+                    stop=True,
                 )
-                neg_max = soft.tile([P, HEADS_PER_BANK], F32)
-                nc.vector.tensor_reduce(out=neg_max[:], in_=masked[:], axis=AXIS.X, op=ALU.max, negate=True)
-                attn = soft.tile([P, HEADS_PER_BANK, T], F32)
-                row_sum = soft.tile([P, HEADS_PER_BANK], F32)
-                for g in range(HEADS_PER_BANK):
-                    nc.scalar.activation(
-                        out=attn[:, g, :], in_=masked[:, g, :], func=ACT.Exp,
-                        bias=neg_max[:, g : g + 1], scale=1.0, accum_out=row_sum[:, g : g + 1],
-                    )
-                inv_sum = soft.tile([P, HEADS_PER_BANK], F32)
-                nc.vector.reciprocal(out=inv_sum[:], in_=row_sum[:])
-                nc.vector.tensor_tensor(
-                    out=attn[:], in0=attn[:],
-                    in1=inv_sum[:].unsqueeze(2).to_broadcast([P, HEADS_PER_BANK, T]), op=ALU.mult,
+            masked = soft.tile([P, TILES_PER_BANK, T], F32)
+            nc.vector.tensor_tensor(
+                out=masked[:, :, :width], in0=scores[:, :, :width],
+                in1=mask[:, T - width :].unsqueeze(1).to_broadcast([P, TILES_PER_BANK, width]),
+                op=ALU.add,
+            )
+            neg_max = soft.tile([P, TILES_PER_BANK], F32)
+            nc.vector.tensor_reduce(
+                out=neg_max[:], in_=masked[:, :, :width], axis=AXIS.X, op=ALU.max, negate=True
+            )
+            row_sum = soft.tile([P, TILES_PER_BANK], F32)
+            for g in range(TILES_PER_BANK):
+                nc.scalar.activation(
+                    out=attn[:, g, :width], in_=masked[:, g, :width], func=ACT.Exp,
+                    bias=neg_max[:, g : g + 1], scale=1.0, accum_out=row_sum[:, g : g + 1],
                 )
-                nc.sync.dma_start(
-                    out=out[b, n0 : n0 + HEADS_PER_BANK].rearrange("n t s -> t n s"), in_=attn[:]
-                )
+            inv_sum = soft.tile([P, TILES_PER_BANK], F32)
+            nc.vector.reciprocal(out=inv_sum[:], in_=row_sum[:])
+            nc.gpsimd.tensor_tensor(
+                out=attn[:, :, :width], in0=attn[:, :, :width],
+                in1=inv_sum[:].unsqueeze(2).to_broadcast([P, TILES_PER_BANK, width]), op=ALU.mult,
+            )
+            block_out = out[b0 : b0 + BATCHES_PER_BANK, :, BLOCK * j : BLOCK * (j + 1), :].rearrange(
+                "b (k n) t s -> n t (b k) s", n=STACK
+            )
+            for n in range(STACK):
+                nc.sync.dma_start(out=block_out[n], in_=attn[n * BLOCK : (n + 1) * BLOCK, :, :])
+
+        prepare_h(0)
+        for n in range(H):
+            prepare_a(n)
+        for b0 in range(0, B, BATCHES_PER_BANK):
+            if b0 % CHUNK == 0 and b0 + CHUNK < B:
+                prepare_h(b0 + CHUNK)
+            quantised = [project(b) for b in range(b0, b0 + BATCHES_PER_BANK)]
+            for j in reversed(range(N_BLOCKS)):
+                attend(b0, quantised, j, attn_tiles[(j, (b0 // BATCHES_PER_BANK) % ATTN_BUFS)])

@@ -17,14 +17,16 @@ P = 128
 PACK = 4
 NEG_INF = -1e30
 CHUNK = 4
+N_CHUNKS = B // CHUNK
 
 BLOCK = 32
 N_BLOCKS = T // BLOCK
 STACK = P // BLOCK
-N_STACKS = H // STACK
-TILES_PER_BANK = 4
-BATCHES_PER_BANK = TILES_PER_BANK // N_STACKS
-ATTN_BUFS = 3
+ATTN_BUFS = 2
+
+STEPS = N_CHUNKS * H
+ROUND = STACK
+VECTOR_SHARE = 3
 
 FLOPS = 2 * B * H * T * D * (D + T)
 
@@ -33,50 +35,24 @@ def tile_causalselfattention_pa_kernel(tc, h, A, out):
     nc = tc.nc
     with ExitStack() as ctx:
         const = ctx.enter_context(tc.tile_pool(name="const", bufs=1))
-        a_stage = ctx.enter_context(tc.tile_pool(name="a_stage", bufs=3))
-        ha_stage = ctx.enter_context(tc.tile_pool(name="ha_stage", bufs=4))
+        stage = ctx.enter_context(tc.tile_pool(name="stage", bufs=2))
         soft = ctx.enter_context(tc.tile_pool(name="soft", bufs=4))
-        psum_t = ctx.enter_context(tc.psum_pool(name="psum_t", bufs=2))
-        psum_ha = ctx.enter_context(tc.psum_pool(name="psum_ha", bufs=4))
+        psum_work = ctx.enter_context(tc.psum_pool(name="psum_work", bufs=6))
         psum_sc = ctx.enter_context(tc.psum_pool(name="psum_sc", bufs=2))
+        ctx.enter_context(tc.manual_schedule())
 
         h_raw = const.tile([P, B, D], BF16)
         a_raw = const.tile([P, H, PACK, D], BF16)
 
-        def load_h(b0):
-            nc.sync.dma_start(
-                out=h_raw[:, b0 : b0 + CHUNK, :], in_=h[b0 : b0 + CHUNK].rearrange("b t d -> t b d")
-            )
+        def load_h(chunk):
+            batches = slice(chunk * CHUNK, (chunk + 1) * CHUNK)
+            nc.sync.dma_start(out=h_raw[:, batches, :], in_=h[batches].rearrange("b t d -> t b d"))
 
         load_h(0)
         for n in range(H):
             nc.sync.dma_start(out=a_raw[:, n, :, :], in_=A[n].rearrange("(c p) e -> p c e", p=P))
-        for b0 in range(CHUNK, B, CHUNK):
-            load_h(b0)
-
-        ident = const.tile([P, P], BF16)
-        make_identity(nc, ident[:])
-        ident_f32 = const.tile([P, P], F32)
-        make_identity(nc, ident_f32[:])
-
-        mask_t = const.tile([P, P], F32)
-        nc.gpsimd.memset(mask_t[:], 0.0)
-        nc.gpsimd.affine_select(
-            out=mask_t[:], in_=mask_t[:], compare_op=ALU.is_ge, fill=NEG_INF,
-            base=T - BLOCK, channel_multiplier=-1, pattern=[[0, STACK], [1, BLOCK]],
-        )
-        mask_ps = psum_t.tile([P, P], F32, tag="transposed")
-        nc.tensor.transpose(mask_ps[:], mask_t[:], ident_f32[:])
-        mask = const.tile([P, T], F32)
-        nc.vector.tensor_copy(out=mask[:], in_=mask_ps[:])
-
-        attn_tiles = {}
-        for j in range(N_BLOCKS):
-            for k in range(ATTN_BUFS):
-                attn_tile = const.tile([P, TILES_PER_BANK, T], F32, name="attn_%d_%d" % (j, k))
-                if j < N_BLOCKS - 1:
-                    nc.gpsimd.memset(attn_tile[:, :, BLOCK * (j + 1) :], 0.0)
-                attn_tiles[(j, k)] = attn_tile
+        for chunk in range(1, N_CHUNKS):
+            load_h(chunk)
 
         h_grouped = const.tile([P, B, T, PACK], BF16, align_bytes=64)
         h_codes = const.tile([P, B, T], U32, align_bytes=64)
@@ -84,21 +60,25 @@ def tile_causalselfattention_pa_kernel(tc, h, A, out):
         a_codes = const.tile([P, H, D], U32, align_bytes=64)
         a_scales = const.tile([P, H, D], U8, align_bytes=64)
 
-        def prepare_h(b0):
-            for b in range(b0, b0 + CHUNK):
-                h_t = psum_t.tile([P, PACK, T], BF16, tag="transposed")
-                for c in range(PACK):
-                    nc.tensor.transpose(h_t[:, c, :], h_raw[:, b, c * P : (c + 1) * P], ident[:])
-                nc.any.tensor_copy(out=h_grouped[:, b, :, :], in_=h_t[:].rearrange("p c t -> p t c"))
-            chunk = slice(b0, b0 + CHUNK)
+        ident = const.tile([P, P], BF16)
+        make_identity(nc, ident[:])
+
+        def transpose_h(b, copy):
+            h_t = psum_work.tile([P, PACK, T], BF16, tag="work")
+            for c in range(PACK):
+                nc.tensor.transpose(h_t[:, c, :], h_raw[:, b, c * P : (c + 1) * P], ident[:])
+            copy(out=h_grouped[:, b, :, :], in_=h_t[:].rearrange("p c t -> p t c"))
+
+        def quantise_h(chunk):
+            batches = slice(chunk * CHUNK, (chunk + 1) * CHUNK)
             nc.vector.quantize_mx(
-                out=h_codes[:, chunk, :].rearrange("p b t -> p (b t)").bitcast(FP8X4),
-                scales=h_scales[:, chunk, :].rearrange("p b t -> p (b t)"),
-                in_=h_grouped[:, chunk, :, :].rearrange("p b t c -> p (b t c)"),
+                out=h_codes[:, batches, :].rearrange("p b t -> p (b t)").bitcast(FP8X4),
+                scales=h_scales[:, batches, :].rearrange("p b t -> p (b t)"),
+                in_=h_grouped[:, batches, :, :].rearrange("p b t c -> p (b t c)"),
             )
 
         def prepare_a(n):
-            a_grouped = a_stage.tile([P, D, PACK], BF16, align_bytes=64)
+            a_grouped = stage.tile([P, D, PACK], BF16, align_bytes=64)
             nc.vector.tensor_copy(
                 out=a_grouped[:].rearrange("p (e i) c -> p e c i", i=4),
                 in_=a_raw[:, n, :, :].rearrange("p c (e i) -> p e c i", i=4),
@@ -109,85 +89,157 @@ def tile_causalselfattention_pa_kernel(tc, h, A, out):
                 in_=a_grouped[:].rearrange("p e c -> p (e c)"),
             )
 
-        def project(b):
-            ha_grouped = ha_stage.tile([P, N_STACKS, N_BLOCKS, STACK, BLOCK, PACK], BF16, align_bytes=64)
-            ha_codes = ha_stage.tile([P, N_STACKS, N_BLOCKS, P], U32, align_bytes=64)
-            ha_scales = ha_stage.tile([P, N_STACKS, N_BLOCKS, P], U8, align_bytes=64)
-            for k in range(N_STACKS):
-                for n in range(STACK):
-                    head = k * STACK + n
-                    ha_t = psum_ha.tile([P, PACK, T], F32)
-                    for c in range(PACK):
-                        e_cols = slice(c * P, (c + 1) * P)
-                        nc.tensor.matmul_mx(
-                            out=ha_t[:, c, :],
-                            lhsT=a_codes[:, head, e_cols].bitcast(FP8X4),
-                            lhsT_scale=a_scales[:, head, e_cols],
-                            rhs=h_codes[:, b, :].bitcast(FP8X4),
-                            rhs_scale=h_scales[:, b, :],
-                            start=True,
-                            stop=True,
-                        )
-                    nc.any.tensor_copy(
-                        out=ha_grouped[:, k, :, n, :, :],
-                        in_=ha_t[:].rearrange("p c (j i) -> p j i c", i=BLOCK),
-                    )
-                nc.vector.quantize_mx(
-                    out=ha_codes[:, k, :, :].rearrange("p j r -> p (j r)").bitcast(FP8X4),
-                    scales=ha_scales[:, k, :, :].rearrange("p j r -> p (j r)"),
-                    in_=ha_grouped[:, k, :, :, :, :].rearrange("p j n i c -> p (j n i c)"),
-                )
-            return ha_codes, ha_scales
+        ha_grouped = {}
+        ha_codes = {}
+        ha_scales = {}
 
-        def attend(b0, quantised, j, attn):
-            width = BLOCK * (j + 1)
-            scores = psum_sc.tile([P, TILES_PER_BANK, T], F32)
-            for g in range(TILES_PER_BANK):
-                ha_codes, ha_scales = quantised[g // N_STACKS]
-                b = b0 + g // N_STACKS
+        def project(s):
+            head = s % H
+            if s % ROUND == 0:
+                ha_grouped[s // ROUND] = stage.tile(
+                    [P, CHUNK, N_BLOCKS, STACK, BLOCK, PACK], BF16, align_bytes=64, name="ha_grouped"
+                )
+            for i in range(CHUNK):
+                b = (s // H) * CHUNK + i
+                ha_t = psum_work.tile([P, PACK, T], F32, tag="work")
+                for c in range(PACK):
+                    e_cols = slice(c * P, (c + 1) * P)
+                    nc.tensor.matmul_mx(
+                        out=ha_t[:, c, :],
+                        lhsT=a_codes[:, head, e_cols].bitcast(FP8X4),
+                        lhsT_scale=a_scales[:, head, e_cols],
+                        rhs=h_codes[:, b, :].bitcast(FP8X4),
+                        rhs_scale=h_scales[:, b, :],
+                        start=True,
+                        stop=True,
+                    )
+                to_vector = s >= H and (s * CHUNK + i) % VECTOR_SHARE == VECTOR_SHARE - 1
+                copy = nc.vector.tensor_copy if to_vector else nc.scalar.copy
+                copy(
+                    out=ha_grouped[s // ROUND][:, i, :, head % STACK, :, :],
+                    in_=ha_t[:].rearrange("p c (j i) -> p j i c", i=BLOCK),
+                )
+
+        def quantise_ha(m):
+            ha_codes[m] = stage.tile([P, CHUNK, N_BLOCKS, P], U32, align_bytes=64, name="ha_codes")
+            ha_scales[m] = stage.tile([P, CHUNK, N_BLOCKS, P], U8, align_bytes=64, name="ha_scales")
+            for i in range(0, CHUNK, 2):
+                nc.vector.quantize_mx(
+                    out=ha_codes[m][:, i : i + 2, :, :].rearrange("p b j r -> p (b j r)").bitcast(FP8X4),
+                    scales=ha_scales[m][:, i : i + 2, :, :].rearrange("p b j r -> p (b j r)"),
+                    in_=ha_grouped[m][:, i : i + 2, :, :, :, :].rearrange("p b j n i c -> p (b j n i c)"),
+                )
+
+        scores = {}
+        masked = {}
+        neg_max = {}
+        row_sum = {}
+
+        def width_of(a):
+            return BLOCK * (N_BLOCKS - a % ROUND)
+
+        def score(a):
+            m = a // ROUND
+            j = N_BLOCKS - 1 - a % ROUND
+            scores[a] = psum_sc.tile([P, CHUNK, T], F32, name="scores")
+            for i in range(CHUNK):
+                b = (m * ROUND // H) * CHUNK + i
                 nc.tensor.matmul_mx(
-                    out=scores[:, g, :],
-                    lhsT=ha_codes[:, g % N_STACKS, j, :].bitcast(FP8X4),
-                    lhsT_scale=ha_scales[:, g % N_STACKS, j, :],
+                    out=scores[a][:, i, :],
+                    lhsT=ha_codes[m][:, i, j, :].bitcast(FP8X4),
+                    lhsT_scale=ha_scales[m][:, i, j, :],
                     rhs=h_codes[:, b, :].bitcast(FP8X4),
                     rhs_scale=h_scales[:, b, :],
                     start=True,
                     stop=True,
                 )
-            masked = soft.tile([P, TILES_PER_BANK, T], F32)
+
+        def mask_and_max(a):
+            width = width_of(a)
+            masked[a] = soft.tile([P, CHUNK, T], F32, name="masked")
             nc.vector.tensor_tensor(
-                out=masked[:, :, :width], in0=scores[:, :, :width],
-                in1=mask[:, T - width :].unsqueeze(1).to_broadcast([P, TILES_PER_BANK, width]),
-                op=ALU.add,
+                out=masked[a][:, :, :width], in0=scores[a][:, :, :width],
+                in1=mask[:, T - width :].unsqueeze(1).to_broadcast([P, CHUNK, width]), op=ALU.add,
             )
-            neg_max = soft.tile([P, TILES_PER_BANK], F32)
+            neg_max[a] = soft.tile([P, CHUNK], F32, name="neg_max")
             nc.vector.tensor_reduce(
-                out=neg_max[:], in_=masked[:, :, :width], axis=AXIS.X, op=ALU.max, negate=True
+                out=neg_max[a][:], in_=masked[a][:, :, :width], axis=AXIS.X, op=ALU.max, negate=True
             )
-            row_sum = soft.tile([P, TILES_PER_BANK], F32)
-            for g in range(TILES_PER_BANK):
+
+        def attn_of(a):
+            return attn_tiles[(a % ROUND, (a // ROUND) % ATTN_BUFS)]
+
+        def exponentials(a):
+            width = width_of(a)
+            row_sum[a] = soft.tile([P, CHUNK], F32, name="row_sum")
+            for i in range(CHUNK):
                 nc.scalar.activation(
-                    out=attn[:, g, :width], in_=masked[:, g, :width], func=ACT.Exp,
-                    bias=neg_max[:, g : g + 1], scale=1.0, accum_out=row_sum[:, g : g + 1],
+                    out=attn_of(a)[:, i, :width], in_=masked[a][:, i, :width], func=ACT.Exp,
+                    bias=neg_max[a][:, i : i + 1], scale=1.0, accum_out=row_sum[a][:, i : i + 1],
                 )
-            inv_sum = soft.tile([P, TILES_PER_BANK], F32)
-            nc.vector.reciprocal(out=inv_sum[:], in_=row_sum[:])
+
+        def scale_and_store(a):
+            width = width_of(a)
+            m = a // ROUND
+            j = N_BLOCKS - 1 - a % ROUND
+            attn = attn_of(a)
+            inv_sum = soft.tile([P, CHUNK], F32)
+            nc.vector.reciprocal(out=inv_sum[:], in_=row_sum[a][:])
             nc.gpsimd.tensor_tensor(
                 out=attn[:, :, :width], in0=attn[:, :, :width],
-                in1=inv_sum[:].unsqueeze(2).to_broadcast([P, TILES_PER_BANK, width]), op=ALU.mult,
+                in1=inv_sum[:].unsqueeze(2).to_broadcast([P, CHUNK, width]), op=ALU.mult,
             )
-            block_out = out[b0 : b0 + BATCHES_PER_BANK, :, BLOCK * j : BLOCK * (j + 1), :].rearrange(
-                "b (k n) t s -> n t (b k) s", n=STACK
-            )
+            b0 = (m * ROUND // H) * CHUNK
             for n in range(STACK):
-                nc.sync.dma_start(out=block_out[n], in_=attn[n * BLOCK : (n + 1) * BLOCK, :, :])
+                head = (m * ROUND) % H + n
+                nc.sync.dma_start(
+                    out=out[b0 : b0 + CHUNK, head, BLOCK * j : BLOCK * (j + 1), :].rearrange("b t s -> t b s"),
+                    in_=attn[n * BLOCK : (n + 1) * BLOCK, :, :],
+                )
 
-        prepare_h(0)
+        for i in range(CHUNK):
+            transpose_h(i, nc.vector.tensor_copy if i % 2 else nc.scalar.copy)
+        quantise_h(0)
         for n in range(H):
             prepare_a(n)
-        for b0 in range(0, B, BATCHES_PER_BANK):
-            if b0 % CHUNK == 0 and b0 + CHUNK < B:
-                prepare_h(b0 + CHUNK)
-            quantised = [project(b) for b in range(b0, b0 + BATCHES_PER_BANK)]
-            for j in reversed(range(N_BLOCKS)):
-                attend(b0, quantised, j, attn_tiles[(j, (b0 // BATCHES_PER_BANK) % ATTN_BUFS)])
+
+        ident_f32 = const.tile([P, P], F32)
+        make_identity(nc, ident_f32[:])
+        mask_t = const.tile([P, P], F32)
+        nc.gpsimd.memset(mask_t[:], 0.0)
+        nc.gpsimd.affine_select(
+            out=mask_t[:], in_=mask_t[:], compare_op=ALU.is_ge, fill=NEG_INF,
+            base=T - BLOCK, channel_multiplier=-1, pattern=[[0, STACK], [1, BLOCK]],
+        )
+        mask_ps = psum_sc.tile([P, P], F32, tag="scores")
+        nc.tensor.transpose(mask_ps[:], mask_t[:], ident_f32[:])
+        mask = const.tile([P, T], F32)
+        nc.vector.tensor_copy(out=mask[:], in_=mask_ps[:])
+
+        attn_tiles = {}
+        for x in range(ROUND):
+            for k in range(ATTN_BUFS):
+                attn_tile = const.tile([P, CHUNK, T], F32, name="attn_%d_%d" % (x, k))
+                if x > 0:
+                    nc.gpsimd.memset(attn_tile[:, :, BLOCK * (N_BLOCKS - x) :], 0.0)
+                attn_tiles[(x, k)] = attn_tile
+
+        for s in range(STEPS + ROUND + 5):
+            if s % ROUND == 0 and 0 < s <= STEPS:
+                quantise_ha(s // ROUND - 1)
+            if s < STEPS:
+                project(s)
+            if 0 <= s - ROUND - 1 < STEPS:
+                score(s - ROUND - 1)
+            if 0 <= s - ROUND - 2 < STEPS:
+                mask_and_max(s - ROUND - 2)
+            if 0 <= s - ROUND - 3 < STEPS:
+                exponentials(s - ROUND - 3)
+            if 0 <= s - ROUND - 4 < STEPS:
+                scale_and_store(s - ROUND - 4)
+            next_chunk = s // H + 1
+            i = s % H - (H - CHUNK - 1)
+            if next_chunk < N_CHUNKS and 0 <= i < CHUNK:
+                transpose_h(next_chunk * CHUNK + i, nc.scalar.copy)
+            if next_chunk < N_CHUNKS and s % H == H - 1:
+                quantise_h(next_chunk)

@@ -6,6 +6,7 @@ from concourse.masks import make_identity
 FP8X4 = mybir.dt.float8_e4m3fn_x4
 BF16 = mybir.dt.bfloat16
 F32 = mybir.dt.float32
+I32 = mybir.dt.int32
 U32 = mybir.dt.uint32
 U8 = mybir.dt.uint8
 ALU = mybir.AluOpType
@@ -22,11 +23,8 @@ N_CHUNKS = B // CHUNK
 BLOCK = 32
 N_BLOCKS = T // BLOCK
 STACK = P // BLOCK
-ATTN_BUFS = 2
-
-STEPS = N_CHUNKS * H
-ROUND = STACK
-VECTOR_SHARE = 3
+N_STACKS = H // STACK
+ATTN_BUFS = 3
 
 FLOPS = 2 * B * H * T * D * (D + T)
 
@@ -35,11 +33,11 @@ def tile_causalselfattention_pa_kernel(tc, h, A, out):
     nc = tc.nc
     with ExitStack() as ctx:
         const = ctx.enter_context(tc.tile_pool(name="const", bufs=1))
-        stage = ctx.enter_context(tc.tile_pool(name="stage", bufs=2))
+        a_stage = ctx.enter_context(tc.tile_pool(name="a_stage", bufs=3))
+        ha_stage = ctx.enter_context(tc.tile_pool(name="ha_stage", bufs=6))
         soft = ctx.enter_context(tc.tile_pool(name="soft", bufs=4))
         psum_work = ctx.enter_context(tc.psum_pool(name="psum_work", bufs=6))
         psum_sc = ctx.enter_context(tc.psum_pool(name="psum_sc", bufs=2))
-        ctx.enter_context(tc.manual_schedule())
 
         h_raw = const.tile([P, B, D], BF16)
         a_raw = const.tile([P, H, PACK, D], BF16)
@@ -50,196 +48,162 @@ def tile_causalselfattention_pa_kernel(tc, h, A, out):
 
         load_h(0)
         for n in range(H):
-            nc.sync.dma_start(out=a_raw[:, n, :, :], in_=A[n].rearrange("(c p) e -> p c e", p=P))
+            nc.sync.dma_start(
+                out=a_raw[:, n, :, :].rearrange("p (u x) e -> p u x e", x=2),
+                in_=A[n].rearrange("(u p x) e -> p u x e", p=P, x=2),
+            )
         for chunk in range(1, N_CHUNKS):
             load_h(chunk)
 
-        h_grouped = const.tile([P, B, T, PACK], BF16, align_bytes=64)
-        h_codes = const.tile([P, B, T], U32, align_bytes=64)
-        h_scales = const.tile([P, B, T], U8, align_bytes=64)
-        a_codes = const.tile([P, H, D], U32, align_bytes=64)
-        a_scales = const.tile([P, H, D], U8, align_bytes=64)
-
-        ident = const.tile([P, P], BF16)
-        make_identity(nc, ident[:])
-
-        def transpose_h(b, copy):
-            h_t = psum_work.tile([P, PACK, T], BF16, tag="work")
-            for c in range(PACK):
-                nc.tensor.transpose(h_t[:, c, :], h_raw[:, b, c * P : (c + 1) * P], ident[:])
-            copy(out=h_grouped[:, b, :, :], in_=h_t[:].rearrange("p c t -> p t c"))
-
-        def quantise_h(chunk):
-            batches = slice(chunk * CHUNK, (chunk + 1) * CHUNK)
-            nc.vector.quantize_mx(
-                out=h_codes[:, batches, :].rearrange("p b t -> p (b t)").bitcast(FP8X4),
-                scales=h_scales[:, batches, :].rearrange("p b t -> p (b t)"),
-                in_=h_grouped[:, batches, :, :].rearrange("p b t c -> p (b t c)"),
-            )
-
-        def prepare_a(n):
-            a_grouped = stage.tile([P, D, PACK], BF16, align_bytes=64)
-            nc.vector.tensor_copy(
-                out=a_grouped[:].rearrange("p (e i) c -> p e c i", i=4),
-                in_=a_raw[:, n, :, :].rearrange("p c (e i) -> p e c i", i=4),
-            )
-            nc.vector.quantize_mx(
-                out=a_codes[:, n, :].bitcast(FP8X4),
-                scales=a_scales[:, n, :],
-                in_=a_grouped[:].rearrange("p e c -> p (e c)"),
-            )
-
-        ha_grouped = {}
-        ha_codes = {}
-        ha_scales = {}
-
-        def project(s):
-            head = s % H
-            if s % ROUND == 0:
-                ha_grouped[s // ROUND] = stage.tile(
-                    [P, CHUNK, N_BLOCKS, STACK, BLOCK, PACK], BF16, align_bytes=64, name="ha_grouped"
-                )
-            for i in range(CHUNK):
-                b = (s // H) * CHUNK + i
-                ha_t = psum_work.tile([P, PACK, T], F32, tag="work")
-                for c in range(PACK):
-                    e_cols = slice(c * P, (c + 1) * P)
-                    nc.tensor.matmul_mx(
-                        out=ha_t[:, c, :],
-                        lhsT=a_codes[:, head, e_cols].bitcast(FP8X4),
-                        lhsT_scale=a_scales[:, head, e_cols],
-                        rhs=h_codes[:, b, :].bitcast(FP8X4),
-                        rhs_scale=h_scales[:, b, :],
-                        start=True,
-                        stop=True,
-                    )
-                to_vector = s >= H and (s * CHUNK + i) % VECTOR_SHARE == VECTOR_SHARE - 1
-                copy = nc.vector.tensor_copy if to_vector else nc.scalar.copy
-                copy(
-                    out=ha_grouped[s // ROUND][:, i, :, head % STACK, :, :],
-                    in_=ha_t[:].rearrange("p c (j i) -> p j i c", i=BLOCK),
-                )
-
-        def quantise_ha(m):
-            ha_codes[m] = stage.tile([P, CHUNK, N_BLOCKS, P], U32, align_bytes=64, name="ha_codes")
-            ha_scales[m] = stage.tile([P, CHUNK, N_BLOCKS, P], U8, align_bytes=64, name="ha_scales")
-            for i in range(0, CHUNK, 2):
-                nc.vector.quantize_mx(
-                    out=ha_codes[m][:, i : i + 2, :, :].rearrange("p b j r -> p (b j r)").bitcast(FP8X4),
-                    scales=ha_scales[m][:, i : i + 2, :, :].rearrange("p b j r -> p (b j r)"),
-                    in_=ha_grouped[m][:, i : i + 2, :, :, :, :].rearrange("p b j n i c -> p (b j n i c)"),
-                )
-
-        scores = {}
-        masked = {}
-        neg_max = {}
-        row_sum = {}
-
-        def width_of(a):
-            return BLOCK * (N_BLOCKS - a % ROUND)
-
-        def score(a):
-            m = a // ROUND
-            j = N_BLOCKS - 1 - a % ROUND
-            scores[a] = psum_sc.tile([P, CHUNK, T], F32, name="scores")
-            for i in range(CHUNK):
-                b = (m * ROUND // H) * CHUNK + i
-                nc.tensor.matmul_mx(
-                    out=scores[a][:, i, :],
-                    lhsT=ha_codes[m][:, i, j, :].bitcast(FP8X4),
-                    lhsT_scale=ha_scales[m][:, i, j, :],
-                    rhs=h_codes[:, b, :].bitcast(FP8X4),
-                    rhs_scale=h_scales[:, b, :],
-                    start=True,
-                    stop=True,
-                )
-
-        def mask_and_max(a):
-            width = width_of(a)
-            masked[a] = soft.tile([P, CHUNK, T], F32, name="masked")
-            nc.vector.tensor_tensor(
-                out=masked[a][:, :, :width], in0=scores[a][:, :, :width],
-                in1=mask[:, T - width :].unsqueeze(1).to_broadcast([P, CHUNK, width]), op=ALU.add,
-            )
-            neg_max[a] = soft.tile([P, CHUNK], F32, name="neg_max")
-            nc.vector.tensor_reduce(
-                out=neg_max[a][:], in_=masked[a][:, :, :width], axis=AXIS.X, op=ALU.max, negate=True
-            )
-
-        def attn_of(a):
-            return attn_tiles[(a % ROUND, (a // ROUND) % ATTN_BUFS)]
-
-        def exponentials(a):
-            width = width_of(a)
-            row_sum[a] = soft.tile([P, CHUNK], F32, name="row_sum")
-            for i in range(CHUNK):
-                nc.scalar.activation(
-                    out=attn_of(a)[:, i, :width], in_=masked[a][:, i, :width], func=ACT.Exp,
-                    bias=neg_max[a][:, i : i + 1], scale=1.0, accum_out=row_sum[a][:, i : i + 1],
-                )
-
-        def scale_and_store(a):
-            width = width_of(a)
-            m = a // ROUND
-            j = N_BLOCKS - 1 - a % ROUND
-            attn = attn_of(a)
-            inv_sum = soft.tile([P, CHUNK], F32)
-            nc.vector.reciprocal(out=inv_sum[:], in_=row_sum[a][:])
-            nc.gpsimd.tensor_tensor(
-                out=attn[:, :, :width], in0=attn[:, :, :width],
-                in1=inv_sum[:].unsqueeze(2).to_broadcast([P, CHUNK, width]), op=ALU.mult,
-            )
-            b0 = (m * ROUND // H) * CHUNK
-            for n in range(STACK):
-                head = (m * ROUND) % H + n
-                nc.sync.dma_start(
-                    out=out[b0 : b0 + CHUNK, head, BLOCK * j : BLOCK * (j + 1), :].rearrange("b t s -> t b s"),
-                    in_=attn[n * BLOCK : (n + 1) * BLOCK, :, :],
-                )
-
-        for i in range(CHUNK):
-            transpose_h(i, nc.vector.tensor_copy if i % 2 else nc.scalar.copy)
-        quantise_h(0)
-        for n in range(H):
-            prepare_a(n)
-
         ident_f32 = const.tile([P, P], F32)
         make_identity(nc, ident_f32[:])
+
         mask_t = const.tile([P, P], F32)
         nc.gpsimd.memset(mask_t[:], 0.0)
         nc.gpsimd.affine_select(
             out=mask_t[:], in_=mask_t[:], compare_op=ALU.is_ge, fill=NEG_INF,
             base=T - BLOCK, channel_multiplier=-1, pattern=[[0, STACK], [1, BLOCK]],
         )
-        mask_ps = psum_sc.tile([P, P], F32, tag="scores")
+        mask_ps = psum_work.tile([P, P], F32, tag="work")
         nc.tensor.transpose(mask_ps[:], mask_t[:], ident_f32[:])
         mask = const.tile([P, T], F32)
         nc.vector.tensor_copy(out=mask[:], in_=mask_ps[:])
 
         attn_tiles = {}
-        for x in range(ROUND):
+        for j in range(N_BLOCKS):
             for k in range(ATTN_BUFS):
-                attn_tile = const.tile([P, CHUNK, T], F32, name="attn_%d_%d" % (x, k))
-                if x > 0:
-                    nc.gpsimd.memset(attn_tile[:, :, BLOCK * (N_BLOCKS - x) :], 0.0)
-                attn_tiles[(x, k)] = attn_tile
+                attn_tile = const.tile([P, CHUNK, T], F32, name="attn_%d_%d" % (j, k))
+                if j < N_BLOCKS - 1:
+                    nc.gpsimd.memset(attn_tile[:, :, BLOCK * (j + 1) :], 0.0)
+                attn_tiles[(j, k)] = attn_tile
 
-        for s in range(STEPS + ROUND + 5):
-            if s % ROUND == 0 and 0 < s <= STEPS:
-                quantise_ha(s // ROUND - 1)
-            if s < STEPS:
-                project(s)
-            if 0 <= s - ROUND - 1 < STEPS:
-                score(s - ROUND - 1)
-            if 0 <= s - ROUND - 2 < STEPS:
-                mask_and_max(s - ROUND - 2)
-            if 0 <= s - ROUND - 3 < STEPS:
-                exponentials(s - ROUND - 3)
-            if 0 <= s - ROUND - 4 < STEPS:
-                scale_and_store(s - ROUND - 4)
-            next_chunk = s // H + 1
-            i = s % H - (H - CHUNK - 1)
-            if next_chunk < N_CHUNKS and 0 <= i < CHUNK:
-                transpose_h(next_chunk * CHUNK + i, nc.scalar.copy)
-            if next_chunk < N_CHUNKS and s % H == H - 1:
-                quantise_h(next_chunk)
+        h_grouped = const.tile([P, B, T, PACK], BF16, align_bytes=64)
+        h_codes = const.tile([P, B, T], U32, align_bytes=64)
+        h_scales = const.tile([P, B, T], U8, align_bytes=64)
+        hb_codes = const.tile([P, N_CHUNKS, N_BLOCKS, CHUNK * BLOCK], U32, align_bytes=64)
+        hb_scales = const.tile([P, N_CHUNKS, N_BLOCKS, CHUNK * BLOCK], U8, align_bytes=64)
+        a_codes = const.tile([P, H, D], U32, align_bytes=64)
+        a_scales = const.tile([P, H, D], U8, align_bytes=64)
+        nc.vector.memset(h_scales[:].bitcast(I32), 0)
+
+        def prepare_h(chunk):
+            b0 = chunk * CHUNK
+            for b in range(b0, b0 + CHUNK, 2):
+                h_t = psum_work.tile([P, 2, 2, T], F32, tag="work")
+                for i in range(2):
+                    words = h_raw[:, b + i, :].bitcast(F32)
+                    for u in range(2):
+                        nc.tensor.transpose(h_t[:, i, u, :], words[:, u * P : (u + 1) * P], ident_f32[:])
+                nc.scalar.copy(
+                    out=h_grouped[:, b : b + 2, :, :].bitcast(F32), in_=h_t[:].rearrange("p b u t -> p b t u")
+                )
+            batches = slice(b0, b0 + CHUNK)
+            nc.vector.quantize_mx(
+                out=h_codes[:, batches, :].rearrange("p b t -> p (b t)").bitcast(FP8X4),
+                scales=h_scales[:, batches, :].rearrange("p b t -> p (b t)"),
+                in_=h_grouped[:, batches, :, :].rearrange("p b t c -> p (b t c)"),
+            )
+            nc.vector.tensor_copy(
+                out=hb_codes[:, chunk, :, :].bitcast(I32).rearrange("p j (b i) -> p j b i", b=CHUNK),
+                in_=h_codes[:, batches, :].bitcast(I32).rearrange("p b (j i) -> p j b i", j=N_BLOCKS),
+            )
+            nc.vector.tensor_copy(
+                out=hb_scales[:, chunk, :, :].bitcast(I32).rearrange("p j (b w) -> p j b w", b=CHUNK),
+                in_=h_scales[:, batches, :].bitcast(I32).rearrange("p b (j w) -> p j b w", j=N_BLOCKS),
+            )
+
+        def prepare_a(n):
+            a_grouped = a_stage.tile([P, PACK, P, PACK], BF16, align_bytes=64)
+            for u in range(2):
+                nc.vector.tensor_copy(
+                    out=a_grouped[:, 2 * u : 2 * u + 2, :, :].rearrange("p x (m i) c -> p m c i x", i=2),
+                    in_=a_raw[:, n, :, 2 * u * P : 2 * (u + 1) * P].rearrange("p c (m i x) -> p m c i x", i=2, x=2),
+                )
+            nc.vector.quantize_mx(
+                out=a_codes[:, n, :].bitcast(FP8X4),
+                scales=a_scales[:, n, :],
+                in_=a_grouped[:].rearrange("p k m c -> p (k m c)"),
+            )
+
+        def project(chunk, stack, j):
+            ha_grouped = ha_stage.tile([P, CHUNK, STACK, BLOCK, PACK], BF16, align_bytes=64)
+            for n in range(STACK):
+                head = stack * STACK + n
+                ha_t = psum_work.tile([P, PACK, CHUNK * BLOCK], F32, tag="work")
+                for c in range(PACK):
+                    e_cols = slice(c * P, (c + 1) * P)
+                    nc.tensor.matmul_mx(
+                        out=ha_t[:, c, :],
+                        lhsT=a_codes[:, head, e_cols].bitcast(FP8X4),
+                        lhsT_scale=a_scales[:, head, e_cols],
+                        rhs=hb_codes[:, chunk, j, :].bitcast(FP8X4),
+                        rhs_scale=hb_scales[:, chunk, j, :],
+                        start=True,
+                        stop=True,
+                    )
+                nc.any.tensor_copy(
+                    out=ha_grouped[:, :, n, :, :], in_=ha_t[:].rearrange("p c (b i) -> p b i c", b=CHUNK)
+                )
+            ha_codes = ha_stage.tile([P, CHUNK, P], U32, align_bytes=64)
+            ha_scales = ha_stage.tile([P, CHUNK, P], U8, align_bytes=64)
+            nc.vector.quantize_mx(
+                out=ha_codes[:].rearrange("p b r -> p (b r)").bitcast(FP8X4),
+                scales=ha_scales[:].rearrange("p b r -> p (b r)"),
+                in_=ha_grouped[:].rearrange("p b n i c -> p (b n i c)"),
+            )
+            return ha_codes, ha_scales
+
+        def attend(chunk, stack, j, ha_codes, ha_scales, attn):
+            width = BLOCK * (j + 1)
+            b0 = chunk * CHUNK
+            scores = psum_sc.tile([P, CHUNK, T], F32)
+            for i in range(CHUNK):
+                nc.tensor.matmul_mx(
+                    out=scores[:, i, :],
+                    lhsT=ha_codes[:, i, :].bitcast(FP8X4),
+                    lhsT_scale=ha_scales[:, i, :],
+                    rhs=h_codes[:, b0 + i, :].bitcast(FP8X4),
+                    rhs_scale=h_scales[:, b0 + i, :],
+                    start=True,
+                    stop=True,
+                )
+            masked = soft.tile([P, CHUNK, T], F32)
+            nc.vector.tensor_tensor(
+                out=masked[:, :, :width], in0=scores[:, :, :width],
+                in1=mask[:, T - width :].unsqueeze(1).to_broadcast([P, CHUNK, width]), op=ALU.add,
+            )
+            neg_max = soft.tile([P, CHUNK], F32)
+            nc.vector.tensor_reduce(
+                out=neg_max[:], in_=masked[:, :, :width], axis=AXIS.X, op=ALU.max, negate=True
+            )
+            row_sum = soft.tile([P, CHUNK], F32)
+            for i in range(CHUNK):
+                nc.scalar.activation(
+                    out=attn[:, i, :width], in_=masked[:, i, :width], func=ACT.Exp,
+                    bias=neg_max[:, i : i + 1], scale=1.0, accum_out=row_sum[:, i : i + 1],
+                )
+            inv_sum = soft.tile([P, CHUNK], F32)
+            nc.vector.reciprocal(out=inv_sum[:], in_=row_sum[:])
+            nc.gpsimd.tensor_tensor(
+                out=attn[:, :, :width], in0=attn[:, :, :width],
+                in1=inv_sum[:].unsqueeze(2).to_broadcast([P, CHUNK, width]), op=ALU.mult,
+            )
+            for n in range(STACK):
+                nc.sync.dma_start(
+                    out=out[b0 : b0 + CHUNK, stack * STACK + n, BLOCK * j : BLOCK * (j + 1), :].rearrange(
+                        "b t s -> t b s"
+                    ),
+                    in_=attn[n * BLOCK : (n + 1) * BLOCK, :, :],
+                )
+
+        prepare_h(0)
+        for n in range(H):
+            prepare_a(n)
+        for chunk in range(N_CHUNKS):
+            if chunk + 1 < N_CHUNKS:
+                prepare_h(chunk + 1)
+            for stack in range(N_STACKS):
+                for j in reversed(range(N_BLOCKS)):
+                    ha_codes, ha_scales = project(chunk, stack, j)
+                    attn = attn_tiles[(j, (chunk * N_STACKS + stack) % ATTN_BUFS)]
+                    attend(chunk, stack, j, ha_codes, ha_scales, attn)

@@ -184,10 +184,11 @@ def tile_causalselfattention_pa_kernel(tc, h, A, out):
                 )
             inv_sum = soft.tile([P, CHUNK], F32)
             nc.vector.reciprocal(out=inv_sum[:], in_=row_sum[:])
-            nc.gpsimd.tensor_tensor(
-                out=attn[:, :, :width], in0=attn[:, :, :width],
-                in1=inv_sum[:].unsqueeze(2).to_broadcast([P, CHUNK, width]), op=ALU.mult,
-            )
+            for i in range(CHUNK):
+                nc.gpsimd.tensor_scalar(
+                    out=attn[:, i, :width], in0=attn[:, i, :width],
+                    scalar1=inv_sum[:, i : i + 1], scalar2=0.0, op0=ALU.mult, op1=ALU.add,
+                )
             for n in range(STACK):
                 nc.sync.dma_start(
                     out=out[b0 : b0 + CHUNK, stack * STACK + n, BLOCK * j : BLOCK * (j + 1), :].rearrange(

@@ -46,14 +46,19 @@ def tile_causalselfattention_pa_kernel(tc, h, A, out):
             batches = slice(chunk * CHUNK, (chunk + 1) * CHUNK)
             nc.sync.dma_start(out=h_raw[:, batches, :], in_=h[batches].rearrange("b t d -> t b d"))
 
-        load_h(0)
-        for n in range(H):
+        def load_a(n):
             nc.sync.dma_start(
                 out=a_raw[:, n, :, :].rearrange("p (u x) e -> p u x e", x=2),
                 in_=A[n].rearrange("(u p x) e -> p u x e", p=P, x=2),
             )
+
+        load_h(0)
+        for n in range(STACK):
+            load_a(n)
         for chunk in range(1, N_CHUNKS):
             load_h(chunk)
+        for n in range(STACK, H):
+            load_a(n)
 
         ident_f32 = const.tile([P, P], F32)
         make_identity(nc, ident_f32[:])
@@ -86,7 +91,7 @@ def tile_causalselfattention_pa_kernel(tc, h, A, out):
         a_scales = const.tile([P, H, D], U8, align_bytes=64)
         nc.vector.memset(h_scales[:].bitcast(I32), 0)
 
-        def prepare_h(chunk):
+        def transpose_h(chunk):
             b0 = chunk * CHUNK
             for b in range(b0, b0 + CHUNK, 2):
                 h_t = psum_work.tile([P, 2, 2, T], F32, tag="work")
@@ -97,7 +102,9 @@ def tile_causalselfattention_pa_kernel(tc, h, A, out):
                 nc.scalar.copy(
                     out=h_grouped[:, b : b + 2, :, :].bitcast(F32), in_=h_t[:].rearrange("p b u t -> p b t u")
                 )
-            batches = slice(b0, b0 + CHUNK)
+
+        def quantize_h(chunk):
+            batches = slice(chunk * CHUNK, (chunk + 1) * CHUNK)
             nc.vector.quantize_mx(
                 out=h_codes[:, batches, :].rearrange("p b t -> p (b t)").bitcast(FP8X4),
                 scales=h_scales[:, batches, :].rearrange("p b t -> p (b t)"),
@@ -112,38 +119,43 @@ def tile_causalselfattention_pa_kernel(tc, h, A, out):
                 in_=h_scales[:, batches, :].bitcast(I32).rearrange("p b (j w) -> p j b w", j=N_BLOCKS),
             )
 
-        def prepare_a(n):
+        def group_a(n):
             a_grouped = a_stage.tile([P, PACK, P, PACK], BF16, align_bytes=64)
             for u in range(2):
                 nc.vector.tensor_copy(
                     out=a_grouped[:, 2 * u : 2 * u + 2, :, :].rearrange("p x (m i) c -> p m c i x", i=2),
                     in_=a_raw[:, n, :, 2 * u * P : 2 * (u + 1) * P].rearrange("p c (m i x) -> p m c i x", i=2, x=2),
                 )
+            return a_grouped
+
+        def quantize_a(n, a_grouped):
             nc.vector.quantize_mx(
                 out=a_codes[:, n, :].bitcast(FP8X4),
                 scales=a_scales[:, n, :],
                 in_=a_grouped[:].rearrange("p k m c -> p (k m c)"),
             )
 
-        def project(chunk, stack, j):
-            ha_grouped = ha_stage.tile([P, CHUNK, STACK, BLOCK, PACK], BF16, align_bytes=64)
-            for n in range(STACK):
-                head = stack * STACK + n
-                ha_t = psum_work.tile([P, PACK, CHUNK * BLOCK], F32, tag="work")
-                for c in range(PACK):
-                    e_cols = slice(c * P, (c + 1) * P)
-                    nc.tensor.matmul_mx(
-                        out=ha_t[:, c, :],
-                        lhsT=a_codes[:, head, e_cols].bitcast(FP8X4),
-                        lhsT_scale=a_scales[:, head, e_cols],
-                        rhs=hb_codes[:, chunk, j, :].bitcast(FP8X4),
-                        rhs_scale=hb_scales[:, chunk, j, :],
-                        start=True,
-                        stop=True,
-                    )
-                nc.any.tensor_copy(
-                    out=ha_grouped[:, :, n, :, :], in_=ha_t[:].rearrange("p c (b i) -> p b i c", b=CHUNK)
+        def project(chunk, stack, j, n, ha_grouped, copy):
+            head = stack * STACK + n
+            ha_t = psum_work.tile([P, PACK, CHUNK * BLOCK], F32, tag="work")
+            for c in range(PACK):
+                e_cols = slice(c * P, (c + 1) * P)
+                nc.tensor.matmul_mx(
+                    out=ha_t[:, c, :],
+                    lhsT=a_codes[:, head, e_cols].bitcast(FP8X4),
+                    lhsT_scale=a_scales[:, head, e_cols],
+                    rhs=hb_codes[:, chunk, j, :].bitcast(FP8X4),
+                    rhs_scale=hb_scales[:, chunk, j, :],
+                    start=True,
+                    stop=True,
                 )
+            copy(out=ha_grouped[:, :, n, :, :], in_=ha_t[:].rearrange("p c (b i) -> p b i c", b=CHUNK))
+
+        def new_grouped():
+            ha_grouped = ha_stage.tile([P, CHUNK, STACK, BLOCK, PACK], BF16, align_bytes=64)
+            return ha_grouped
+
+        def quantize_ha(ha_grouped):
             ha_codes = ha_stage.tile([P, CHUNK, P], U32, align_bytes=64)
             ha_scales = ha_stage.tile([P, CHUNK, P], U8, align_bytes=64)
             nc.vector.quantize_mx(
@@ -197,14 +209,31 @@ def tile_causalselfattention_pa_kernel(tc, h, A, out):
                     in_=attn[n * BLOCK : (n + 1) * BLOCK, :, :],
                 )
 
-        prepare_h(0)
-        for n in range(H):
-            prepare_a(n)
-        for chunk in range(N_CHUNKS):
-            if chunk + 1 < N_CHUNKS:
-                prepare_h(chunk + 1)
-            for stack in range(N_STACKS):
+        first_grouped = [new_grouped() for j in range(N_BLOCKS)]
+        with tc.manual_schedule(engines={mybir.EngineType.DVE}):
+            transpose_h(0)
+            for n in range(STACK):
+                a_grouped = group_a(n)
+                if n == 0:
+                    quantize_h(0)
+                quantize_a(n, a_grouped)
                 for j in reversed(range(N_BLOCKS)):
-                    ha_codes, ha_scales = project(chunk, stack, j)
-                    attn = attn_tiles[(j, (chunk * N_STACKS + stack) % ATTN_BUFS)]
+                    project(0, 0, j, n, first_grouped[j], nc.scalar.copy)
+
+        for stack in range(N_STACKS):
+            for chunk in range(N_CHUNKS):
+                if stack == 0:
+                    if chunk + 1 < N_CHUNKS:
+                        transpose_h(chunk + 1)
+                        quantize_h(chunk + 1)
+                    quantize_a(STACK + chunk, group_a(STACK + chunk))
+                for j in reversed(range(N_BLOCKS)):
+                    if stack == 0 and chunk == 0:
+                        ha_grouped = first_grouped[j]
+                    else:
+                        ha_grouped = new_grouped()
+                        for n in range(STACK):
+                            project(chunk, stack, j, n, ha_grouped, nc.any.tensor_copy)
+                    ha_codes, ha_scales = quantize_ha(ha_grouped)
+                    attn = attn_tiles[(j, (stack * N_CHUNKS + chunk) % ATTN_BUFS)]
                     attend(chunk, stack, j, ha_codes, ha_scales, attn)

@@ -201,7 +201,7 @@ def tile_causalselfattention_pa_kernel(tc, h, A, out):
                     out=attn[:, i, :width], in0=attn[:, i, :width],
                     scalar1=inv_sum[:, i : i + 1], scalar2=0.0, op0=ALU.mult, op1=ALU.add,
                 )
-            for n in range(STACK):
+            for n in (0, 2, 1, 3):
                 nc.sync.dma_start(
                     out=out[b0 : b0 + CHUNK, stack * STACK + n, BLOCK * j : BLOCK * (j + 1), :].rearrange(
                         "b t s -> t b s"

@@ -33,7 +33,7 @@ def tile_causalselfattention_pa_kernel(tc, h, A, out):
     nc = tc.nc
     with ExitStack() as ctx:
         const = ctx.enter_context(tc.tile_pool(name="const", bufs=1))
-        a_stage = ctx.enter_context(tc.tile_pool(name="a_stage", bufs=3))
+        a_stage = ctx.enter_context(tc.tile_pool(name="a_stage", bufs=4))
         ha_stage = ctx.enter_context(tc.tile_pool(name="ha_stage", bufs=6))
         soft = ctx.enter_context(tc.tile_pool(name="soft", bufs=4))
         psum_work = ctx.enter_context(tc.psum_pool(name="psum_work", bufs=6))
@@ -119,14 +119,15 @@ def tile_causalselfattention_pa_kernel(tc, h, A, out):
                 in_=h_scales[:, batches, :].bitcast(I32).rearrange("p b (j w) -> p j b w", j=N_BLOCKS),
             )
 
-        def group_a(n):
+        def new_a():
             a_grouped = a_stage.tile([P, PACK, P, PACK], BF16, align_bytes=64)
-            for u in range(2):
-                nc.vector.tensor_copy(
-                    out=a_grouped[:, 2 * u : 2 * u + 2, :, :].rearrange("p x (m i) c -> p m c i x", i=2),
-                    in_=a_raw[:, n, :, 2 * u * P : 2 * (u + 1) * P].rearrange("p c (m i x) -> p m c i x", i=2, x=2),
-                )
             return a_grouped
+
+        def group_a(n, a_grouped, u, copy):
+            copy(
+                out=a_grouped[:, 2 * u : 2 * u + 2, :, :].rearrange("p x (m i) c -> p m c i x", i=2),
+                in_=a_raw[:, n, :, 2 * u * P : 2 * (u + 1) * P].rearrange("p c (m i x) -> p m c i x", i=2, x=2),
+            )
 
         def quantize_a(n, a_grouped):
             nc.vector.quantize_mx(
@@ -165,7 +166,7 @@ def tile_causalselfattention_pa_kernel(tc, h, A, out):
             )
             return ha_codes, ha_scales
 
-        def attend(chunk, stack, j, ha_codes, ha_scales, attn):
+        def attend(chunk, stack, j, ha_codes, ha_scales, attn, scaling):
             width = BLOCK * (j + 1)
             b0 = chunk * CHUNK
             scores = psum_sc.tile([P, CHUNK, T], F32)
@@ -197,7 +198,7 @@ def tile_causalselfattention_pa_kernel(tc, h, A, out):
             inv_sum = soft.tile([P, CHUNK], F32)
             nc.vector.reciprocal(out=inv_sum[:], in_=row_sum[:])
             for i in range(CHUNK):
-                nc.gpsimd.tensor_scalar(
+                scaling.tensor_scalar(
                     out=attn[:, i, :width], in0=attn[:, i, :width],
                     scalar1=inv_sum[:, i : i + 1], scalar2=0.0, op0=ALU.mult, op1=ALU.add,
                 )
@@ -209,24 +210,38 @@ def tile_causalselfattention_pa_kernel(tc, h, A, out):
                     in_=attn[n * BLOCK : (n + 1) * BLOCK, :, :],
                 )
 
+        copy_v, copy_s = nc.vector.tensor_copy, nc.scalar.copy
         first_grouped = [new_grouped() for j in range(N_BLOCKS)]
-        with tc.manual_schedule(engines={mybir.EngineType.DVE}):
+        pinned = {mybir.EngineType.PE, mybir.EngineType.DVE, mybir.EngineType.Activation}
+        with tc.manual_schedule(engines=pinned):
             transpose_h(0)
+            a_tiles = [new_a() for n in range(STACK)]
+            for n in (1, 2):
+                group_a(n, a_tiles[n], 1, copy_s)
             for n in range(STACK):
-                a_grouped = group_a(n)
+                group_a(n, a_tiles[n], 0, copy_v)
+                if n in (0, STACK - 1):
+                    group_a(n, a_tiles[n], 1, copy_v)
                 if n == 0:
                     quantize_h(0)
-                quantize_a(n, a_grouped)
+                quantize_a(n, a_tiles[n])
+                if n == STACK - 1:
+                    quantize_h(1)
                 for j in reversed(range(N_BLOCKS)):
-                    project(0, 0, j, n, first_grouped[j], nc.scalar.copy)
+                    project(0, 0, j, n, first_grouped[j], copy_v if n == STACK - 1 else copy_s)
+                if n == 0:
+                    transpose_h(1)
 
         for stack in range(N_STACKS):
             for chunk in range(N_CHUNKS):
                 if stack == 0:
-                    if chunk + 1 < N_CHUNKS:
+                    if 2 <= chunk + 1 < N_CHUNKS:
                         transpose_h(chunk + 1)
                         quantize_h(chunk + 1)
-                    quantize_a(STACK + chunk, group_a(STACK + chunk))
+                    a_grouped = new_a()
+                    for u in range(2):
+                        group_a(STACK + chunk, a_grouped, u, copy_v)
+                    quantize_a(STACK + chunk, a_grouped)
                 for j in reversed(range(N_BLOCKS)):
                     if stack == 0 and chunk == 0:
                         ha_grouped = first_grouped[j]
@@ -236,4 +251,5 @@ def tile_causalselfattention_pa_kernel(tc, h, A, out):
                             project(chunk, stack, j, n, ha_grouped, nc.any.tensor_copy)
                     ha_codes, ha_scales = quantize_ha(ha_grouped)
                     attn = attn_tiles[(j, (stack * N_CHUNKS + chunk) % ATTN_BUFS)]
-                    attend(chunk, stack, j, ha_codes, ha_scales, attn)
+                    last = stack == N_STACKS - 1 and chunk == N_CHUNKS - 1 and j < 3
+                    attend(chunk, stack, j, ha_codes, ha_scales, attn, nc.vector if last else nc.gpsimd)

@@ -216,12 +216,9 @@ def tile_causalselfattention_pa_kernel(tc, h, A, out):
         with tc.manual_schedule(engines=pinned):
             transpose_h(0)
             a_tiles = [new_a() for n in range(STACK)]
-            for n in (1, 2):
-                group_a(n, a_tiles[n], 1, copy_s)
             for n in range(STACK):
-                group_a(n, a_tiles[n], 0, copy_v)
-                if n in (0, STACK - 1):
-                    group_a(n, a_tiles[n], 1, copy_v)
+                for u in range(2):
+                    group_a(n, a_tiles[n], u, copy_v)
                 if n == 0:
                     quantize_h(0)
                 quantize_a(n, a_tiles[n])
@@ -248,7 +245,8 @@ def tile_causalselfattention_pa_kernel(tc, h, A, out):
                     else:
                         ha_grouped = new_grouped()
                         for n in range(STACK):
-                            project(chunk, stack, j, n, ha_grouped, nc.any.tensor_copy)
+                            by_vector = n == STACK - 1 or (n == STACK - 2 and j == 0)
+                            project(chunk, stack, j, n, ha_grouped, copy_v if by_vector else copy_s)
                     ha_codes, ha_scales = quantize_ha(ha_grouped)
                     attn = attn_tiles[(j, (stack * N_CHUNKS + chunk) % ATTN_BUFS)]
                     last = stack == N_STACKS - 1 and chunk == N_CHUNKS - 1 and j < 3

@@ -180,19 +180,23 @@ def tile_causalselfattention_pa_kernel(tc, h, A, out):
                     start=True,
                     stop=True,
                 )
-            masked = soft.tile([P, CHUNK, T], F32)
+            corner = slice(width - BLOCK, width)
+            masked = soft.tile([P, CHUNK, BLOCK], F32)
             nc.vector.tensor_tensor(
-                out=masked[:, :, :width], in0=scores[:, :, :width],
-                in1=mask[:, T - width :].unsqueeze(1).to_broadcast([P, CHUNK, width]), op=ALU.add,
+                out=masked[:], in0=scores[:, :, corner],
+                in1=mask[:, T - BLOCK :].unsqueeze(1).to_broadcast([P, CHUNK, BLOCK]), op=ALU.add,
+            )
+            nc.tensor.matmul(
+                out=scores[:, :, corner], lhsT=ident_f32[:], rhs=masked[:], start=True, stop=True
             )
             neg_max = soft.tile([P, CHUNK], F32)
             nc.vector.tensor_reduce(
-                out=neg_max[:], in_=masked[:, :, :width], axis=AXIS.X, op=ALU.max, negate=True
+                out=neg_max[:], in_=scores[:, :, :width], axis=AXIS.X, op=ALU.max, negate=True
             )
             row_sum = soft.tile([P, CHUNK], F32)
             for i in range(CHUNK):
                 nc.scalar.activation(
-                    out=attn[:, i, :width], in_=masked[:, i, :width], func=ACT.Exp,
+                    out=attn[:, i, :width], in_=scores[:, i, :width], func=ACT.Exp,
                     bias=neg_max[:, i : i + 1], scale=1.0, accum_out=row_sum[:, i : i + 1],
                 )
             inv_sum = soft.tile([P, CHUNK], F32)
@@ -245,8 +249,7 @@ def tile_causalselfattention_pa_kernel(tc, h, A, out):
                     else:
                         ha_grouped = new_grouped()
                         for n in range(STACK):
-                            by_vector = n == STACK - 1 or (n == STACK - 2 and j == 0)
-                            project(chunk, stack, j, n, ha_grouped, copy_v if by_vector else copy_s)
+                            project(chunk, stack, j, n, ha_grouped, nc.any.tensor_copy)
                     ha_codes, ha_scales = quantize_ha(ha_grouped)
                     attn = attn_tiles[(j, (stack * N_CHUNKS + chunk) % ATTN_BUFS)]
                     last = stack == N_STACKS - 1 and chunk == N_CHUNKS - 1 and j < 3

@@ -19,12 +19,14 @@ PACK = 4
 NEG_INF = -1e30
 CHUNK = 4
 N_CHUNKS = B // CHUNK
+LAST_CHUNK = N_CHUNKS - 1
 
 BLOCK = 32
 N_BLOCKS = T // BLOCK
 STACK = P // BLOCK
 N_STACKS = H // STACK
 ATTN_BUFS = 3
+SCALED_BY_VECTOR = 6
 
 FLOPS = 2 * B * H * T * D * (D + T)
 
@@ -42,8 +44,7 @@ def tile_causalselfattention_pa_kernel(tc, h, A, out):
         h_raw = const.tile([P, B, D], BF16)
         a_raw = const.tile([P, H, PACK, D], BF16)
 
-        def load_h(chunk):
-            batches = slice(chunk * CHUNK, (chunk + 1) * CHUNK)
+        def load_h(batches):
             nc.sync.dma_start(out=h_raw[:, batches, :], in_=h[batches].rearrange("b t d -> t b d"))
 
         def load_a(n):
@@ -52,11 +53,13 @@ def tile_causalselfattention_pa_kernel(tc, h, A, out):
                 in_=A[n].rearrange("(u p x) e -> p u x e", p=P, x=2),
             )
 
-        load_h(0)
-        for n in range(STACK):
+        load_a(0)
+        for b in range(0, CHUNK, 2):
+            load_h(slice(b, b + 2))
+        for n in range(1, STACK):
             load_a(n)
         for chunk in range(1, N_CHUNKS):
-            load_h(chunk)
+            load_h(slice(chunk * CHUNK, (chunk + 1) * CHUNK))
         for n in range(STACK, H):
             load_a(n)
 
@@ -110,6 +113,9 @@ def tile_causalselfattention_pa_kernel(tc, h, A, out):
                 scales=h_scales[:, batches, :].rearrange("p b t -> p (b t)"),
                 in_=h_grouped[:, batches, :, :].rearrange("p b t c -> p (b t c)"),
             )
+
+        def sort_h(chunk):
+            batches = slice(chunk * CHUNK, (chunk + 1) * CHUNK)
             nc.vector.tensor_copy(
                 out=hb_codes[:, chunk, :, :].bitcast(I32).rearrange("p j (b i) -> p j b i", b=CHUNK),
                 in_=h_codes[:, batches, :].bitcast(I32).rearrange("p b (j i) -> p j b i", j=N_BLOCKS),
@@ -120,37 +126,38 @@ def tile_causalselfattention_pa_kernel(tc, h, A, out):
             )
 
         def new_a():
-            a_grouped = a_stage.tile([P, PACK, P, PACK], BF16, align_bytes=64)
+            a_grouped = a_stage.tile([P, D, PACK], BF16, align_bytes=64)
             return a_grouped
 
-        def group_a(n, a_grouped, u, copy):
-            copy(
-                out=a_grouped[:, 2 * u : 2 * u + 2, :, :].rearrange("p x (m i) c -> p m c i x", i=2),
-                in_=a_raw[:, n, :, 2 * u * P : 2 * (u + 1) * P].rearrange("p c (m i x) -> p m c i x", i=2, x=2),
+        def group_a(n, a_grouped):
+            nc.vector.tensor_copy(
+                out=a_grouped[:].rearrange("p (x m i) c -> p m c i x", x=2, i=2),
+                in_=a_raw[:, n, :, :].rearrange("p c (m i x) -> p m c i x", i=2, x=2),
             )
 
         def quantize_a(n, a_grouped):
             nc.vector.quantize_mx(
                 out=a_codes[:, n, :].bitcast(FP8X4),
                 scales=a_scales[:, n, :],
-                in_=a_grouped[:].rearrange("p k m c -> p (k m c)"),
+                in_=a_grouped[:].rearrange("p e c -> p (e c)"),
             )
 
-        def project(chunk, stack, j, n, ha_grouped, copy):
+        def project(stack, n, rhs, rhs_scale, dest, copy):
             head = stack * STACK + n
             ha_t = psum_work.tile([P, PACK, CHUNK * BLOCK], F32, tag="work")
             for c in range(PACK):
-                e_cols = slice(c * P, (c + 1) * P)
+                u, x = divmod(c, 2)
+                e_cols = slice((2 * x + u) * P, (2 * x + u + 1) * P)
                 nc.tensor.matmul_mx(
                     out=ha_t[:, c, :],
                     lhsT=a_codes[:, head, e_cols].bitcast(FP8X4),
                     lhsT_scale=a_scales[:, head, e_cols],
-                    rhs=hb_codes[:, chunk, j, :].bitcast(FP8X4),
-                    rhs_scale=hb_scales[:, chunk, j, :],
+                    rhs=rhs.bitcast(FP8X4),
+                    rhs_scale=rhs_scale,
                     start=True,
                     stop=True,
                 )
-            copy(out=ha_grouped[:, :, n, :, :], in_=ha_t[:].rearrange("p c (b i) -> p b i c", b=CHUNK))
+            copy(out=dest, in_=ha_t[:].rearrange("p c (a i) -> p a i c", i=BLOCK))
 
         def new_grouped():
             ha_grouped = ha_stage.tile([P, CHUNK, STACK, BLOCK, PACK], BF16, align_bytes=64)
@@ -162,14 +169,15 @@ def tile_causalselfattention_pa_kernel(tc, h, A, out):
             nc.vector.quantize_mx(
                 out=ha_codes[:].rearrange("p b r -> p (b r)").bitcast(FP8X4),
                 scales=ha_scales[:].rearrange("p b r -> p (b r)"),
-                in_=ha_grouped[:].rearrange("p b n i c -> p (b n i c)"),
+                in_=ha_grouped.rearrange("p b n i c -> p (b n i c)"),
             )
             return ha_codes, ha_scales
 
-        def attend(chunk, stack, j, ha_codes, ha_scales, attn, scaling):
+        def score(unit, ha_codes, ha_scales, pool, tag):
+            stack, chunk, j = unit
             width = BLOCK * (j + 1)
             b0 = chunk * CHUNK
-            scores = psum_sc.tile([P, CHUNK, T], F32)
+            scores = pool.tile([P, CHUNK, T], F32, tag=tag)
             for i in range(CHUNK):
                 nc.tensor.matmul_mx(
                     out=scores[:, i, :],
@@ -189,6 +197,12 @@ def tile_causalselfattention_pa_kernel(tc, h, A, out):
             nc.tensor.matmul(
                 out=scores[:, :, corner], lhsT=ident_f32[:], rhs=masked[:], start=True, stop=True
             )
+            return scores
+
+        def finish(unit, scores, attn, scaling):
+            stack, chunk, j = unit
+            width = BLOCK * (j + 1)
+            b0 = chunk * CHUNK
             neg_max = soft.tile([P, CHUNK], F32)
             nc.vector.tensor_reduce(
                 out=neg_max[:], in_=scores[:, :, :width], axis=AXIS.X, op=ALU.max, negate=True
@@ -215,42 +229,59 @@ def tile_causalselfattention_pa_kernel(tc, h, A, out):
                 )
 
         copy_v, copy_s = nc.vector.tensor_copy, nc.scalar.copy
-        first_grouped = [new_grouped() for j in range(N_BLOCKS)]
+        first_grouped = const.tile([P, N_BLOCKS, CHUNK, STACK, BLOCK, PACK], BF16, align_bytes=64)
         pinned = {mybir.EngineType.PE, mybir.EngineType.DVE, mybir.EngineType.Activation}
         with tc.manual_schedule(engines=pinned):
             transpose_h(0)
             a_tiles = [new_a() for n in range(STACK)]
             for n in range(STACK):
-                for u in range(2):
-                    group_a(n, a_tiles[n], u, copy_v)
+                group_a(n, a_tiles[n])
+                quantize_a(n, a_tiles[n])
                 if n == 0:
                     quantize_h(0)
-                quantize_a(n, a_tiles[n])
                 if n == STACK - 1:
                     quantize_h(1)
-                for j in reversed(range(N_BLOCKS)):
-                    project(0, 0, j, n, first_grouped[j], copy_v if n == STACK - 1 else copy_s)
+                    sort_h(1)
+                for b in range(CHUNK):
+                    copy = copy_v if n == STACK - 1 else copy_s
+                    project(0, n, h_codes[:, b, :], h_scales[:, b, :], first_grouped[:, :, b, n, :, :], copy)
                 if n == 0:
                     transpose_h(1)
 
-        for stack in range(N_STACKS):
-            for chunk in range(N_CHUNKS):
-                if stack == 0:
+        units = [
+            (stack, chunk, j)
+            for stack in range(N_STACKS)
+            for chunk in range(N_CHUNKS)
+            for j in reversed(range(N_BLOCKS))
+        ]
+        grouped = {}
+        for k in range(len(units) + 1):
+            if k < len(units):
+                stack, chunk, j = units[k]
+                if stack == 0 and j == N_BLOCKS - 1:
                     if 2 <= chunk + 1 < N_CHUNKS:
                         transpose_h(chunk + 1)
                         quantize_h(chunk + 1)
+                        sort_h(chunk + 1)
+                    if chunk == LAST_CHUNK:
+                        sort_h(0)
                     a_grouped = new_a()
-                    for u in range(2):
-                        group_a(STACK + chunk, a_grouped, u, copy_v)
+                    group_a(STACK + chunk, a_grouped)
                     quantize_a(STACK + chunk, a_grouped)
-                for j in reversed(range(N_BLOCKS)):
-                    if stack == 0 and chunk == 0:
-                        ha_grouped = first_grouped[j]
-                    else:
-                        ha_grouped = new_grouped()
-                        for n in range(STACK):
-                            project(chunk, stack, j, n, ha_grouped, nc.any.tensor_copy)
-                    ha_codes, ha_scales = quantize_ha(ha_grouped)
-                    attn = attn_tiles[(j, (stack * N_CHUNKS + chunk) % ATTN_BUFS)]
-                    last = stack == N_STACKS - 1 and chunk == N_CHUNKS - 1 and j < 3
-                    attend(chunk, stack, j, ha_codes, ha_scales, attn, nc.vector if last else nc.gpsimd)
+                if k < N_BLOCKS:
+                    grouped[k] = first_grouped[:, j, :, :, :, :]
+                else:
+                    ha_grouped = new_grouped()
+                    for n in range(STACK):
+                        project(
+                            stack, n, hb_codes[:, chunk, j, :], hb_scales[:, chunk, j, :],
+                            ha_grouped[:, :, n, :, :], copy_s if n < 2 else nc.any.tensor_copy,
+                        )
+                    grouped[k] = ha_grouped[:]
+
+            if k >= 1:
+                stack, chunk, j = units[k - 1]
+                pool, tag = (psum_work, "work") if k >= len(units) - 1 else (psum_sc, "scores")
+                scores = score(units[k - 1], *quantize_ha(grouped[k - 1]), pool, tag)
+                attn = attn_tiles[(j, (stack * N_CHUNKS + chunk) % ATTN_BUFS)]
+                finish(units[k - 1], scores, attn, nc.vector if k > len(units) - SCALED_BY_VECTOR else nc.gpsimd)

@@ -114,13 +114,13 @@ def tile_causalselfattention_pa_kernel(tc, h, A, out):
                 in_=h_grouped[:, batches, :, :].rearrange("p b t c -> p (b t c)"),
             )
 
-        def sort_h(chunk):
+        def sort_h(chunk, engine):
             batches = slice(chunk * CHUNK, (chunk + 1) * CHUNK)
-            nc.vector.tensor_copy(
+            engine.tensor_copy(
                 out=hb_codes[:, chunk, :, :].bitcast(I32).rearrange("p j (b i) -> p j b i", b=CHUNK),
                 in_=h_codes[:, batches, :].bitcast(I32).rearrange("p b (j i) -> p j b i", j=N_BLOCKS),
             )
-            nc.vector.tensor_copy(
+            engine.tensor_copy(
                 out=hb_scales[:, chunk, :, :].bitcast(I32).rearrange("p j (b w) -> p j b w", b=CHUNK),
                 in_=h_scales[:, batches, :].bitcast(I32).rearrange("p b (j w) -> p j b w", j=N_BLOCKS),
             )
@@ -241,7 +241,7 @@ def tile_causalselfattention_pa_kernel(tc, h, A, out):
                     quantize_h(0)
                 if n == STACK - 1:
                     quantize_h(1)
-                    sort_h(1)
+                    sort_h(1, nc.vector)
                 for b in range(CHUNK):
                     copy = copy_v if n == STACK - 1 else copy_s
                     project(0, n, h_codes[:, b, :], h_scales[:, b, :], first_grouped[:, :, b, n, :, :], copy)
@@ -262,9 +262,9 @@ def tile_causalselfattention_pa_kernel(tc, h, A, out):
                     if 2 <= chunk + 1 < N_CHUNKS:
                         transpose_h(chunk + 1)
                         quantize_h(chunk + 1)
-                        sort_h(chunk + 1)
+                        sort_h(chunk + 1, nc.gpsimd)
                     if chunk == LAST_CHUNK:
-                        sort_h(0)
+                        sort_h(0, nc.gpsimd)
                     a_grouped = new_a()
                     group_a(STACK + chunk, a_grouped)
                     quantize_a(STACK + chunk, a_grouped)
@@ -275,7 +275,7 @@ def tile_causalselfattention_pa_kernel(tc, h, A, out):
                     for n in range(STACK):
                         project(
                             stack, n, hb_codes[:, chunk, j, :], hb_scales[:, chunk, j, :],
-                            ha_grouped[:, :, n, :, :], copy_s if n < 2 else nc.any.tensor_copy,
+                            ha_grouped[:, :, n, :, :], copy_s if n < (3 if j == N_BLOCKS - 1 else 2) else nc.any.tensor_copy,
                         )
                     grouped[k] = ha_grouped[:]
 

from contextlib import ExitStack

import concourse.mybir as mybir
from concourse.masks import make_identity

FP8X4 = mybir.dt.float8_e4m3fn_x4
BF16 = mybir.dt.bfloat16
F32 = mybir.dt.float32
I32 = mybir.dt.int32
U32 = mybir.dt.uint32
U8 = mybir.dt.uint8
ALU = mybir.AluOpType
ACT = mybir.ActivationFunctionType
AXIS = mybir.AxisListType

B, T, D, H = 16, 128, 512, 8
P = 128
PACK = 4
NEG_INF = -1e30
CHUNK = 4
N_CHUNKS = B // CHUNK
LAST_CHUNK = N_CHUNKS - 1

BLOCK = 32
N_BLOCKS = T // BLOCK
STACK = P // BLOCK
N_STACKS = H // STACK
ATTN_BUFS = 3
SCALED_BY_VECTOR = 6

FLOPS = 2 * B * H * T * D * (D + T)


def tile_causalselfattention_pa_kernel(tc, h, A, out):
    nc = tc.nc
    with ExitStack() as ctx:
        const = ctx.enter_context(tc.tile_pool(name="const", bufs=1))
        a_stage = ctx.enter_context(tc.tile_pool(name="a_stage", bufs=4))
        ha_stage = ctx.enter_context(tc.tile_pool(name="ha_stage", bufs=6))
        soft = ctx.enter_context(tc.tile_pool(name="soft", bufs=4))
        psum_work = ctx.enter_context(tc.psum_pool(name="psum_work", bufs=6))
        psum_sc = ctx.enter_context(tc.psum_pool(name="psum_sc", bufs=2))

        h_raw = const.tile([P, B, D], BF16)
        a_raw = const.tile([P, H, PACK, D], BF16)

        def load_h(batches):
            nc.sync.dma_start(out=h_raw[:, batches, :], in_=h[batches].rearrange("b t d -> t b d"))

        def load_a(n):
            nc.sync.dma_start(
                out=a_raw[:, n, :, :].rearrange("p (u x) e -> p u x e", x=2),
                in_=A[n].rearrange("(u p x) e -> p u x e", p=P, x=2),
            )

        load_a(0)
        for b in range(0, CHUNK, 2):
            load_h(slice(b, b + 2))
        for n in range(1, STACK):
            load_a(n)
        for chunk in range(1, N_CHUNKS):
            load_h(slice(chunk * CHUNK, (chunk + 1) * CHUNK))
        for n in range(STACK, H):
            load_a(n)

        ident_f32 = const.tile([P, P], F32)
        make_identity(nc, ident_f32[:])

        mask_t = const.tile([P, P], F32)
        nc.gpsimd.memset(mask_t[:], 0.0)
        nc.gpsimd.affine_select(
            out=mask_t[:], in_=mask_t[:], compare_op=ALU.is_ge, fill=NEG_INF,
            base=T - BLOCK, channel_multiplier=-1, pattern=[[0, STACK], [1, BLOCK]],
        )
        mask_ps = psum_work.tile([P, P], F32, tag="work")
        nc.tensor.transpose(mask_ps[:], mask_t[:], ident_f32[:])
        mask = const.tile([P, T], F32)
        nc.vector.tensor_copy(out=mask[:], in_=mask_ps[:])

        attn_tiles = {}
        for j in range(N_BLOCKS):
            for k in range(ATTN_BUFS):
                attn_tile = const.tile([P, CHUNK, T], F32, name="attn_%d_%d" % (j, k))
                if j < N_BLOCKS - 1:
                    nc.gpsimd.memset(attn_tile[:, :, BLOCK * (j + 1) :], 0.0)
                attn_tiles[(j, k)] = attn_tile

        h_grouped = const.tile([P, B, T, PACK], BF16, align_bytes=64)
        h_codes = const.tile([P, B, T], U32, align_bytes=64)
        h_scales = const.tile([P, B, T], U8, align_bytes=64)
        hb_codes = const.tile([P, N_CHUNKS, N_BLOCKS, CHUNK * BLOCK], U32, align_bytes=64)
        hb_scales = const.tile([P, N_CHUNKS, N_BLOCKS, CHUNK * BLOCK], U8, align_bytes=64)
        a_codes = const.tile([P, H, D], U32, align_bytes=64)
        a_scales = const.tile([P, H, D], U8, align_bytes=64)
        nc.vector.memset(h_scales[:].bitcast(I32), 0)

        def transpose_h(chunk):
            b0 = chunk * CHUNK
            for b in range(b0, b0 + CHUNK, 2):
                h_t = psum_work.tile([P, 2, 2, T], F32, tag="work")
                for i in range(2):
                    words = h_raw[:, b + i, :].bitcast(F32)
                    for u in range(2):
                        nc.tensor.transpose(h_t[:, i, u, :], words[:, u * P : (u + 1) * P], ident_f32[:])
                nc.scalar.copy(
                    out=h_grouped[:, b : b + 2, :, :].bitcast(F32), in_=h_t[:].rearrange("p b u t -> p b t u")
                )

        def quantize_h(chunk):
            batches = slice(chunk * CHUNK, (chunk + 1) * CHUNK)
            nc.vector.quantize_mx(
                out=h_codes[:, batches, :].rearrange("p b t -> p (b t)").bitcast(FP8X4),
                scales=h_scales[:, batches, :].rearrange("p b t -> p (b t)"),
                in_=h_grouped[:, batches, :, :].rearrange("p b t c -> p (b t c)"),
            )

        def sort_h(chunk, engine):
            batches = slice(chunk * CHUNK, (chunk + 1) * CHUNK)
            engine.tensor_copy(
                out=hb_codes[:, chunk, :, :].bitcast(I32).rearrange("p j (b i) -> p j b i", b=CHUNK),
                in_=h_codes[:, batches, :].bitcast(I32).rearrange("p b (j i) -> p j b i", j=N_BLOCKS),
            )
            engine.tensor_copy(
                out=hb_scales[:, chunk, :, :].bitcast(I32).rearrange("p j (b w) -> p j b w", b=CHUNK),
                in_=h_scales[:, batches, :].bitcast(I32).rearrange("p b (j w) -> p j b w", j=N_BLOCKS),
            )

        def new_a():
            a_grouped = a_stage.tile([P, D, PACK], BF16, align_bytes=64)
            return a_grouped

        def group_a(n, a_grouped):
            nc.vector.tensor_copy(
                out=a_grouped[:].rearrange("p (x m i) c -> p m c i x", x=2, i=2),
                in_=a_raw[:, n, :, :].rearrange("p c (m i x) -> p m c i x", i=2, x=2),
            )

        def quantize_a(n, a_grouped):
            nc.vector.quantize_mx(
                out=a_codes[:, n, :].bitcast(FP8X4),
                scales=a_scales[:, n, :],
                in_=a_grouped[:].rearrange("p e c -> p (e c)"),
            )

        def project(stack, n, rhs, rhs_scale, dest, copy):
            head = stack * STACK + n
            ha_t = psum_work.tile([P, PACK, CHUNK * BLOCK], F32, tag="work")
            for c in range(PACK):
                u, x = divmod(c, 2)
                e_cols = slice((2 * x + u) * P, (2 * x + u + 1) * P)
                nc.tensor.matmul_mx(
                    out=ha_t[:, c, :],
                    lhsT=a_codes[:, head, e_cols].bitcast(FP8X4),
                    lhsT_scale=a_scales[:, head, e_cols],
                    rhs=rhs.bitcast(FP8X4),
                    rhs_scale=rhs_scale,
                    start=True,
                    stop=True,
                )
            copy(out=dest, in_=ha_t[:].rearrange("p c (a i) -> p a i c", i=BLOCK))

        def new_grouped():
            ha_grouped = ha_stage.tile([P, CHUNK, STACK, BLOCK, PACK], BF16, align_bytes=64)
            return ha_grouped

        def quantize_ha(ha_grouped):
            ha_codes = ha_stage.tile([P, CHUNK, P], U32, align_bytes=64)
            ha_scales = ha_stage.tile([P, CHUNK, P], U8, align_bytes=64)
            nc.vector.quantize_mx(
                out=ha_codes[:].rearrange("p b r -> p (b r)").bitcast(FP8X4),
                scales=ha_scales[:].rearrange("p b r -> p (b r)"),
                in_=ha_grouped.rearrange("p b n i c -> p (b n i c)"),
            )
            return ha_codes, ha_scales

        def score(unit, ha_codes, ha_scales, pool, tag):
            stack, chunk, j = unit
            width = BLOCK * (j + 1)
            b0 = chunk * CHUNK
            scores = pool.tile([P, CHUNK, T], F32, tag=tag)
            for i in range(CHUNK):
                nc.tensor.matmul_mx(
                    out=scores[:, i, :],
                    lhsT=ha_codes[:, i, :].bitcast(FP8X4),
                    lhsT_scale=ha_scales[:, i, :],
                    rhs=h_codes[:, b0 + i, :].bitcast(FP8X4),
                    rhs_scale=h_scales[:, b0 + i, :],
                    start=True,
                    stop=True,
                )
            corner = slice(width - BLOCK, width)
            masked = soft.tile([P, CHUNK, BLOCK], F32)
            nc.vector.tensor_tensor(
                out=masked[:], in0=scores[:, :, corner],
                in1=mask[:, T - BLOCK :].unsqueeze(1).to_broadcast([P, CHUNK, BLOCK]), op=ALU.add,
            )
            nc.tensor.matmul(
                out=scores[:, :, corner], lhsT=ident_f32[:], rhs=masked[:], start=True, stop=True
            )
            return scores

        def finish(unit, scores, attn, scaling):
            stack, chunk, j = unit
            width = BLOCK * (j + 1)
            b0 = chunk * CHUNK
            neg_max = soft.tile([P, CHUNK], F32)
            nc.vector.tensor_reduce(
                out=neg_max[:], in_=scores[:, :, :width], axis=AXIS.X, op=ALU.max, negate=True
            )
            row_sum = soft.tile([P, CHUNK], F32)
            for i in range(CHUNK):
                nc.scalar.activation(
                    out=attn[:, i, :width], in_=scores[:, i, :width], func=ACT.Exp,
                    bias=neg_max[:, i : i + 1], scale=1.0, accum_out=row_sum[:, i : i + 1],
                )
            inv_sum = soft.tile([P, CHUNK], F32)
            nc.vector.reciprocal(out=inv_sum[:], in_=row_sum[:])
            for i in range(CHUNK):
                scaling.tensor_scalar(
                    out=attn[:, i, :width], in0=attn[:, i, :width],
                    scalar1=inv_sum[:, i : i + 1], scalar2=0.0, op0=ALU.mult, op1=ALU.add,
                )
            for n in (0, 2, 1, 3):
                nc.sync.dma_start(
                    out=out[b0 : b0 + CHUNK, stack * STACK + n, BLOCK * j : BLOCK * (j + 1), :].rearrange(
                        "b t s -> t b s"
                    ),
                    in_=attn[n * BLOCK : (n + 1) * BLOCK, :, :],
                )

        copy_v, copy_s = nc.vector.tensor_copy, nc.scalar.copy
        first_grouped = const.tile([P, N_BLOCKS, CHUNK, STACK, BLOCK, PACK], BF16, align_bytes=64)
        pinned = {mybir.EngineType.PE, mybir.EngineType.DVE, mybir.EngineType.Activation}
        with tc.manual_schedule(engines=pinned):
            transpose_h(0)
            a_tiles = [new_a() for n in range(STACK)]
            for n in range(STACK):
                group_a(n, a_tiles[n])
                quantize_a(n, a_tiles[n])
                if n == 0:
                    quantize_h(0)
                if n == STACK - 1:
                    quantize_h(1)
                    sort_h(1, nc.vector)
                for b in range(CHUNK):
                    copy = copy_v if n == STACK - 1 else copy_s
                    project(0, n, h_codes[:, b, :], h_scales[:, b, :], first_grouped[:, :, b, n, :, :], copy)
                if n == 0:
                    transpose_h(1)

        units = [
            (stack, chunk, j)
            for stack in range(N_STACKS)
            for chunk in range(N_CHUNKS)
            for j in reversed(range(N_BLOCKS))
        ]
        grouped = {}
        for k in range(len(units) + 1):
            if k < len(units):
                stack, chunk, j = units[k]
                if stack == 0 and j == N_BLOCKS - 1:
                    if 2 <= chunk + 1 < N_CHUNKS:
                        transpose_h(chunk + 1)
                        quantize_h(chunk + 1)
                        sort_h(chunk + 1, nc.gpsimd)
                    if chunk == LAST_CHUNK:
                        sort_h(0, nc.gpsimd)
                    a_grouped = new_a()
                    group_a(STACK + chunk, a_grouped)
                    quantize_a(STACK + chunk, a_grouped)
                if k < N_BLOCKS:
                    grouped[k] = first_grouped[:, j, :, :, :, :]
                else:
                    ha_grouped = new_grouped()
                    for n in range(STACK):
                        project(
                            stack, n, hb_codes[:, chunk, j, :], hb_scales[:, chunk, j, :],
                            ha_grouped[:, :, n, :, :], copy_s if n < (3 if j == N_BLOCKS - 1 else 2) else nc.any.tensor_copy,
                        )
                    grouped[k] = ha_grouped[:]

            if k >= 1:
                stack, chunk, j = units[k - 1]
                pool, tag = (psum_work, "work") if k >= len(units) - 1 else (psum_sc, "scores")
                scores = score(units[k - 1], *quantize_ha(grouped[k - 1]), pool, tag)
                attn = attn_tiles[(j, (stack * N_CHUNKS + chunk) % ATTN_BUFS)]
                finish(units[k - 1], scores, attn, nc.vector if k > len(units) - SCALED_BY_VECTOR else nc.gpsimd)
